import numpy as np
import ml_dtypes


def mxq(x, axis, fmt="e4m3"):
    dtype, down = {"e4m3": (ml_dtypes.float8_e4m3fn, 7), "e5m2": (ml_dtypes.float8_e5m2, 14)}[fmt]
    v = np.moveaxis(np.asarray(x, np.float32).astype(ml_dtypes.bfloat16).astype(np.float64), axis, -1)
    blocks = v.reshape(v.shape[:-1] + (-1, 32))
    amax = np.abs(blocks).max(-1, keepdims=True)
    byte = np.maximum(np.where(amax > 0, np.frexp(amax)[1] - 1 + 127, 0) - down, 1)
    scale = np.exp2(byte - 127.0)
    codes = (blocks / scale).astype(np.float32).astype(dtype).astype(np.float64)
    return np.moveaxis((codes * scale).reshape(v.shape), -1, axis)


BF16 = ml_dtypes.bfloat16


def bf(x):
    return np.asarray(x, np.float32).astype(BF16)


def f64(x):
    return np.asarray(x).astype(np.float64)


B, C, H, W, R = 2, 512, 64, 32, 4
N = H * W
NOISE = 0.5


def mix(a, z):
    return sum(a[:, :, r, None] * z[:, r, None, :] for r in range(R))


def softmax(s):
    e = np.exp(s - s.max(-1, keepdims=True))
    return e / e.sum(-1, keepdims=True)


def setup_inputs():
    z = np.random.standard_normal((B, R, N))
    a1 = np.random.standard_normal((B, C, R)) / np.sqrt(R)
    a2 = np.random.standard_normal((B, C, R)) / np.sqrt(R)
    x1 = mix(a1, z) + NOISE * np.random.standard_normal((B, C, N))
    x2 = mix(a2, z) + NOISE * np.random.standard_normal((B, C, N))
    u1 = a1 / np.sqrt((a1 * a1).sum(2, keepdims=True) + NOISE * NOISE)
    u2 = a2 / np.sqrt((a2 * a2).sum(2, keepdims=True) + NOISE * NOISE)
    logits1 = mix(u1 + u2, u1.transpose(0, 2, 1))
    logits2 = mix(u2 + u1, u2.transpose(0, 2, 1))
    return {"logits1": bf(logits1), "logits2": bf(logits2),
            "x1": bf(x1.reshape(B, C, H, W)), "x2": bf(x2.reshape(B, C, H, W))}


def reference(logits1, logits2, x1, x2):
    x1f = f64(x1)
    x2f = f64(x2)
    x111 = x1f.reshape(B, C, N)
    x211 = x2f.reshape(B, C, N)
    attn11 = softmax(f64(logits1))
    attn22 = softmax(f64(logits2))
    y1 = mxq(attn11, 2, "e4m3") @ mxq(x111, 1, "e4m3")
    y2 = mxq(attn22, 2, "e4m3") @ mxq(x211, 1, "e4m3")
    x1_o = y1.transpose(0, 2, 1).reshape(B, C, H, W) + x1f
    x2_o = y2.transpose(0, 2, 1).reshape(B, C, H, W) + x2f
    return x1_o + x2_o

@@ -1,0 +1,170 @@
+from contextlib import ExitStack
+
+import concourse.mybir as mybir
+from concourse.masks import make_identity
+
+F32 = mybir.dt.float32
+BF16 = mybir.dt.bfloat16
+U32 = mybir.dt.uint32
+U8 = mybir.dt.uint8
+FP8X4 = mybir.dt.float8_e4m3fn_x4
+ALU = mybir.AluOpType
+ACT = mybir.ActivationFunctionType
+AXIS = mybir.AxisListType
+
+P = 128
+PACK = 4
+BATCH = 2
+STREAMS = 2
+C = 512
+N = 2048
+ROW_TILES = C // P
+QUARTERS = N // C
+CHUNK = N // PACK
+VECTOR_EVERY = 4
+
+FLOPS = 2 * STREAMS * BATCH * C * C * N
+
+
+def softmax_rows(nc, work, small, scores):
+    neg_max = small.tile([P, ROW_TILES], F32, name="neg_max")
+    nc.vector.tensor_reduce(out=neg_max[:], in_=scores[:], axis=AXIS.X, op=ALU.max, negate=True)
+    exps = work.tile([P, ROW_TILES, C], F32, name="exps")
+    row_sum = small.tile([P, ROW_TILES], F32, name="row_sum")
+    for a in range(ROW_TILES):
+        nc.scalar.activation(
+            out=exps[:, a, :],
+            in_=scores[:, a, :],
+            func=ACT.Exp,
+            bias=neg_max[:, a : a + 1],
+            scale=1.0,
+            accum_out=row_sum[:, a : a + 1],
+        )
+    inv_sum = small.tile([P, ROW_TILES], F32, name="inv_sum")
+    nc.vector.reciprocal(out=inv_sum[:], in_=row_sum[:])
+    probs = work.tile([P, ROW_TILES, C], BF16, name="probs")
+    for a in range(ROW_TILES):
+        nc.vector.tensor_scalar(
+            out=probs[:, a, :],
+            in0=exps[:, a, :],
+            scalar1=inv_sum[:, a : a + 1],
+            scalar2=None,
+            op0=ALU.mult,
+        )
+    return probs
+
+
+def quantise_probs(nc, work, turn_banks, identity, probs, codes, scales):
+    grouped = work.tile([P, C, PACK], BF16, name="p_grouped", align_bytes=64)
+    for half in range(2):
+        turned = turn_banks.tile([P, 2, PACK, P], BF16, name="turned")
+        for a in range(2):
+            for t in range(PACK):
+                nc.tensor.transpose(
+                    turned[:, a, t, :],
+                    probs[:, 2 * half + a, t * P : (t + 1) * P],
+                    identity[:],
+                )
+        nc.scalar.copy(
+            out=grouped[:, 2 * half * P : 2 * (half + 1) * P, :].rearrange(
+                "q (a c) t -> q a c t", a=2
+            ),
+            in_=turned[:].rearrange("q a t c -> q a c t"),
+        )
+    nc.vector.quantize_mx(
+        out=codes.bitcast(FP8X4),
+        scales=scales,
+        in_=grouped[:].rearrange("q c t -> q (c t)"),
+    )
+
+
+def quantise_map_chunk(nc, work, on_vector, x_map, chunk, codes, scales):
+    cols = slice(chunk * CHUNK, (chunk + 1) * CHUNK)
+    grouped = work.tile([P, PACK * CHUNK], BF16, name="x_grouped", align_bytes=64)
+    source = x_map[:, :, cols].rearrange("p t (m r) -> p m t r", r=QUARTERS)
+    target = grouped[:].rearrange("p (r m t) -> p m t r", r=QUARTERS, t=PACK)
+    if on_vector:
+        nc.vector.tensor_copy(out=target, in_=source)
+    else:
+        nc.scalar.copy(out=target, in_=source)
+    nc.vector.quantize_mx(
+        out=codes[:, cols].bitcast(FP8X4), scales=scales[:, cols], in_=grouped[:]
+    )
+
+
+def tile_interfusion_pb_kernel(tc, logits1, logits2, x1, x2, out):
+    nc = tc.nc
+    logits = (logits1, logits2)
+    maps = (x1, x2)
+    with ExitStack() as stack:
+        keep = stack.enter_context(tc.tile_pool(name="keep", bufs=1))
+        work = stack.enter_context(tc.tile_pool(name="work", bufs=2))
+        regroup = stack.enter_context(tc.tile_pool(name="regroup", bufs=4))
+        small = stack.enter_context(tc.tile_pool(name="small", bufs=4))
+        results = stack.enter_context(tc.tile_pool(name="results", bufs=3))
+        turn_banks = stack.enter_context(tc.psum_pool(name="turn_banks", bufs=2))
+        sum_banks = stack.enter_context(tc.psum_pool(name="sum_banks", bufs=6))
+
+        scores = {}
+        x_maps = {}
+        for b in range(BATCH):
+            for s in range(STREAMS):
+                scores[b, s] = keep.tile([P, ROW_TILES, C], BF16, name="scores_%d_%d" % (b, s))
+                nc.sync.dma_start(
+                    out=scores[b, s][:], in_=logits[s][b].rearrange("(a p) k -> p a k", p=P)
+                )
+            for s in range(STREAMS):
+                x_maps[b, s] = keep.tile([P, PACK, N], BF16, name="x_map_%d_%d" % (b, s))
+                nc.sync.dma_start(
+                    out=x_maps[b, s][:], in_=maps[s][b].rearrange("(t p) h w -> p t (h w)", p=P)
+                )
+
+        identity = keep.tile([P, P], BF16, name="identity")
+        make_identity(nc, identity[:])
+
+        for b in range(BATCH):
+            p_codes = {}
+            p_scales = {}
+            x_codes = {}
+            x_scales = {}
+            for s in range(STREAMS):
+                p_codes[s] = work.tile([P, C], U32, name="p_codes_%d" % s, align_bytes=64)
+                p_scales[s] = work.tile([P, C], U8, name="p_scales_%d" % s, align_bytes=64)
+                x_codes[s] = work.tile([P, N], U32, name="x_codes_%d" % s, align_bytes=64)
+                x_scales[s] = work.tile([P, N], U8, name="x_scales_%d" % s, align_bytes=64)
+            for s in range(STREAMS):
+                probs = softmax_rows(nc, work, small, scores[b, s])
+                quantise_probs(
+                    nc, work, turn_banks, identity, probs, p_codes[s][:], p_scales[s][:]
+                )
+            for chunk in range(PACK):
+                for s in range(STREAMS):
+                    on_vector = (chunk * STREAMS + s) % VECTOR_EVERY == 0
+                    quantise_map_chunk(
+                        nc, regroup, on_vector, x_maps[b, s], chunk, x_codes[s], x_scales[s]
+                    )
+            for j in range(PACK):
+                total = results.tile([P, N], F32, name="total")
+                nc.gpsimd.tensor_tensor(
+                    out=total[:], in0=x_maps[b, 0][:, j, :], in1=x_maps[b, 1][:, j, :], op=ALU.add
+                )
+                for r in range(QUARTERS):
+                    m_cols = slice(j * CHUNK + r * P, j * CHUNK + (r + 1) * P)
+                    c_cols = slice(r * C, (r + 1) * C)
+                    sums = sum_banks.tile([P, C], F32, name="sums")
+                    for s in range(STREAMS):
+                        nc.tensor.matmul_mx(
+                            out=sums[:],
+                            lhsT=x_codes[s][:, m_cols].bitcast(FP8X4),
+                            lhsT_scale=x_scales[s][:, m_cols],
+                            rhs=p_codes[s][:].bitcast(FP8X4),
+                            rhs_scale=p_scales[s][:],
+                            start=(s == 0),
+                            stop=(s == STREAMS - 1),
+                        )
+                    nc.vector.tensor_tensor(
+                        out=total[:, c_cols], in0=sums[:], in1=total[:, c_cols], op=ALU.add
+                    )
+                nc.sync.dma_start(
+                    out=out[b, j * P : (j + 1) * P].rearrange("m h w -> m (h w)"), in_=total[:]
+                )

@@ -21,14 +21,29 @@ N = 2048
 ROW_TILES = C // P
 QUARTERS = N // C
 CHUNK = N // PACK
-VECTOR_EVERY = 4
+FOLDED = 64
 
 FLOPS = 2 * STREAMS * BATCH * C * C * N
 
 
 def softmax_rows(nc, work, small, scores):
+    folded = work.tile([P, ROW_TILES, C // 2], BF16, name="folded")
+    nc.vector.tensor_tensor(
+        out=folded[:], in0=scores[:, :, : C // 2], in1=scores[:, :, C // 2 :], op=ALU.max
+    )
+    width = C // 4
+    while width >= FOLDED:
+        nc.vector.tensor_tensor(
+            out=folded[:, :, :width],
+            in0=folded[:, :, :width],
+            in1=folded[:, :, width : 2 * width],
+            op=ALU.max,
+        )
+        width //= 2
     neg_max = small.tile([P, ROW_TILES], F32, name="neg_max")
-    nc.vector.tensor_reduce(out=neg_max[:], in_=scores[:], axis=AXIS.X, op=ALU.max, negate=True)
+    nc.vector.tensor_reduce(
+        out=neg_max[:], in_=folded[:, :, :FOLDED], axis=AXIS.X, op=ALU.max, negate=True
+    )
     exps = work.tile([P, ROW_TILES, C], F32, name="exps")
     row_sum = small.tile([P, ROW_TILES], F32, name="row_sum")
     for a in range(ROW_TILES):
@@ -44,13 +59,18 @@ def softmax_rows(nc, work, small, scores):
     nc.vector.reciprocal(out=inv_sum[:], in_=row_sum[:])
     probs = work.tile([P, ROW_TILES, C], BF16, name="probs")
     for a in range(ROW_TILES):
-        nc.vector.tensor_scalar(
-            out=probs[:, a, :],
-            in0=exps[:, a, :],
-            scalar1=inv_sum[:, a : a + 1],
-            scalar2=None,
-            op0=ALU.mult,
-        )
+        if a % 2 == 0:
+            nc.vector.tensor_scalar(
+                out=probs[:, a, :],
+                in0=exps[:, a, :],
+                scalar1=inv_sum[:, a : a + 1],
+                scalar2=None,
+                op0=ALU.mult,
+            )
+        else:
+            nc.scalar.activation(
+                out=probs[:, a, :], in_=exps[:, a, :], func=ACT.Copy, scale=inv_sum[:, a : a + 1]
+            )
     return probs
 
 
@@ -101,7 +121,7 @@ def tile_interfusion_pb_kernel(tc, logits1, logits2, x1, x2, out):
         work = stack.enter_context(tc.tile_pool(name="work", bufs=2))
         regroup = stack.enter_context(tc.tile_pool(name="regroup", bufs=4))
         small = stack.enter_context(tc.tile_pool(name="small", bufs=4))
-        results = stack.enter_context(tc.tile_pool(name="results", bufs=3))
+        results = stack.enter_context(tc.tile_pool(name="results", bufs=6))
         turn_banks = stack.enter_context(tc.psum_pool(name="turn_banks", bufs=2))
         sum_banks = stack.enter_context(tc.psum_pool(name="sum_banks", bufs=6))
 
@@ -115,9 +135,12 @@ def tile_interfusion_pb_kernel(tc, logits1, logits2, x1, x2, out):
                 )
             for s in range(STREAMS):
                 x_maps[b, s] = keep.tile([P, PACK, N], BF16, name="x_map_%d_%d" % (b, s))
-                nc.sync.dma_start(
-                    out=x_maps[b, s][:], in_=maps[s][b].rearrange("(t p) h w -> p t (h w)", p=P)
-                )
+            for t in range(PACK):
+                for s in range(STREAMS):
+                    nc.sync.dma_start(
+                        out=x_maps[b, s][:, t, :],
+                        in_=maps[s][b, t * P : (t + 1) * P].rearrange("p h w -> p (h w)"),
+                    )
 
         identity = keep.tile([P, P], BF16, name="identity")
         make_identity(nc, identity[:])
@@ -137,17 +160,23 @@ def tile_interfusion_pb_kernel(tc, logits1, logits2, x1, x2, out):
                 quantise_probs(
                     nc, work, turn_banks, identity, probs, p_codes[s][:], p_scales[s][:]
                 )
+            totals = {}
+            for j in range(PACK):
+                totals[j] = results.tile([P, N], F32, name="total")
+                nc.vector.tensor_tensor(
+                    out=totals[j][:],
+                    in0=x_maps[b, 0][:, j, :],
+                    in1=x_maps[b, 1][:, j, :],
+                    op=ALU.add,
+                )
             for chunk in range(PACK):
                 for s in range(STREAMS):
-                    on_vector = (chunk * STREAMS + s) % VECTOR_EVERY == 0
+                    on_vector = chunk == PACK - 1
                     quantise_map_chunk(
                         nc, regroup, on_vector, x_maps[b, s], chunk, x_codes[s], x_scales[s]
                     )
             for j in range(PACK):
-                total = results.tile([P, N], F32, name="total")
-                nc.gpsimd.tensor_tensor(
-                    out=total[:], in0=x_maps[b, 0][:, j, :], in1=x_maps[b, 1][:, j, :], op=ALU.add
-                )
+                total = totals[j]
                 for r in range(QUARTERS):
                     m_cols = slice(j * CHUNK + r * P, j * CHUNK + (r + 1) * P)
                     c_cols = slice(r * C, (r + 1) * C)
@@ -165,6 +194,7 @@ def tile_interfusion_pb_kernel(tc, logits1, logits2, x1, x2, out):
                     nc.vector.tensor_tensor(
                         out=total[:, c_cols], in0=sums[:], in1=total[:, c_cols], op=ALU.add
                     )
-                nc.sync.dma_start(
-                    out=out[b, j * P : (j + 1) * P].rearrange("m h w -> m (h w)"), in_=total[:]
-                )
+                    nc.sync.dma_start(
+                        out=out[b, j * P : (j + 1) * P].rearrange("m h w -> m (h w)")[:, c_cols],
+                        in_=total[:, c_cols],
+                    )

@@ -21,12 +21,13 @@ N = 2048
 ROW_TILES = C // P
 QUARTERS = N // C
 CHUNK = N // PACK
+GPSIMD_QUARTERS = 2
 FOLDED = 64
 
 FLOPS = 2 * STREAMS * BATCH * C * C * N
 
 
-def softmax_rows(nc, work, small, scores):
+def negated_row_maxima(nc, work, small, scores):
     folded = work.tile([P, ROW_TILES, C // 2], BF16, name="folded")
     nc.vector.tensor_tensor(
         out=folded[:], in0=scores[:, :, : C // 2], in1=scores[:, :, C // 2 :], op=ALU.max
@@ -44,6 +45,10 @@ def softmax_rows(nc, work, small, scores):
     nc.vector.tensor_reduce(
         out=neg_max[:], in_=folded[:, :, :FOLDED], axis=AXIS.X, op=ALU.max, negate=True
     )
+    return neg_max
+
+
+def softmax_rows(nc, work, small, scores, neg_max):
     exps = work.tile([P, ROW_TILES, C], F32, name="exps")
     row_sum = small.tile([P, ROW_TILES], F32, name="row_sum")
     for a in range(ROW_TILES):
@@ -59,18 +64,9 @@ def softmax_rows(nc, work, small, scores):
     nc.vector.reciprocal(out=inv_sum[:], in_=row_sum[:])
     probs = work.tile([P, ROW_TILES, C], BF16, name="probs")
     for a in range(ROW_TILES):
-        if a % 2 == 0:
-            nc.vector.tensor_scalar(
-                out=probs[:, a, :],
-                in0=exps[:, a, :],
-                scalar1=inv_sum[:, a : a + 1],
-                scalar2=None,
-                op0=ALU.mult,
-            )
-        else:
-            nc.scalar.activation(
-                out=probs[:, a, :], in_=exps[:, a, :], func=ACT.Copy, scale=inv_sum[:, a : a + 1]
-            )
+        nc.scalar.activation(
+            out=probs[:, a, :], in_=exps[:, a, :], func=ACT.Copy, scale=inv_sum[:, a : a + 1]
+        )
     return probs
 
 
@@ -100,7 +96,12 @@ def quantise_probs(nc, work, turn_banks, identity, probs, codes, scales):
 
 def quantise_map_chunk(nc, work, on_vector, x_map, chunk, codes, scales):
     cols = slice(chunk * CHUNK, (chunk + 1) * CHUNK)
-    grouped = work.tile([P, PACK * CHUNK], BF16, name="x_grouped", align_bytes=64)
+    grouped = work.tile(
+        [P, PACK * CHUNK],
+        BF16,
+        name="x_grouped_vector" if on_vector else "x_grouped_scalar",
+        align_bytes=64,
+    )
     source = x_map[:, :, cols].rearrange("p t (m r) -> p m t r", r=QUARTERS)
     target = grouped[:].rearrange("p (r m t) -> p m t r", r=QUARTERS, t=PACK)
     if on_vector:
@@ -119,7 +120,7 @@ def tile_interfusion_pb_kernel(tc, logits1, logits2, x1, x2, out):
     with ExitStack() as stack:
         keep = stack.enter_context(tc.tile_pool(name="keep", bufs=1))
         work = stack.enter_context(tc.tile_pool(name="work", bufs=2))
-        regroup = stack.enter_context(tc.tile_pool(name="regroup", bufs=4))
+        regroup = stack.enter_context(tc.tile_pool(name="regroup", bufs=2))
         small = stack.enter_context(tc.tile_pool(name="small", bufs=4))
         results = stack.enter_context(tc.tile_pool(name="results", bufs=6))
         turn_banks = stack.enter_context(tc.psum_pool(name="turn_banks", bufs=2))
@@ -145,54 +146,80 @@ def tile_interfusion_pb_kernel(tc, logits1, logits2, x1, x2, out):
         identity = keep.tile([P, P], BF16, name="identity")
         make_identity(nc, identity[:])
 
+        p_codes = {}
+        p_scales = {}
+
+        neg_maxima = {}
+
+        def row_maxima(b):
+            for s in range(STREAMS):
+                neg_maxima[b, s] = negated_row_maxima(nc, work, small, scores[b, s])
+
+        def quantised_softmax(b):
+            for s in range(STREAMS):
+                p_codes[b, s] = work.tile([P, C], U32, name="p_codes_%d" % s, align_bytes=64)
+                p_scales[b, s] = work.tile([P, C], U8, name="p_scales_%d" % s, align_bytes=64)
+                probs = softmax_rows(nc, work, small, scores[b, s], neg_maxima[b, s])
+                quantise_probs(
+                    nc, work, turn_banks, identity, probs, p_codes[b, s][:], p_scales[b, s][:]
+                )
+
+        row_maxima(0)
+        quantised_softmax(0)
         for b in range(BATCH):
-            p_codes = {}
-            p_scales = {}
+            if b + 1 < BATCH:
+                row_maxima(b + 1)
             x_codes = {}
             x_scales = {}
             for s in range(STREAMS):
-                p_codes[s] = work.tile([P, C], U32, name="p_codes_%d" % s, align_bytes=64)
-                p_scales[s] = work.tile([P, C], U8, name="p_scales_%d" % s, align_bytes=64)
                 x_codes[s] = work.tile([P, N], U32, name="x_codes_%d" % s, align_bytes=64)
                 x_scales[s] = work.tile([P, N], U8, name="x_scales_%d" % s, align_bytes=64)
-            for s in range(STREAMS):
-                probs = softmax_rows(nc, work, small, scores[b, s])
-                quantise_probs(
-                    nc, work, turn_banks, identity, probs, p_codes[s][:], p_scales[s][:]
-                )
             totals = {}
             for j in range(PACK):
                 totals[j] = results.tile([P, N], F32, name="total")
+                for r in range(GPSIMD_QUARTERS):
+                    c_cols = slice(r * C, (r + 1) * C)
+                    nc.gpsimd.tensor_tensor(
+                        out=totals[j][:, c_cols],
+                        in0=x_maps[b, 0][:, j, c_cols],
+                        in1=x_maps[b, 1][:, j, c_cols],
+                        op=ALU.add,
+                    )
+                rest = slice(GPSIMD_QUARTERS * C, N)
                 nc.vector.tensor_tensor(
-                    out=totals[j][:],
-                    in0=x_maps[b, 0][:, j, :],
-                    in1=x_maps[b, 1][:, j, :],
+                    out=totals[j][:, rest],
+                    in0=x_maps[b, 0][:, j, rest],
+                    in1=x_maps[b, 1][:, j, rest],
                     op=ALU.add,
                 )
             for chunk in range(PACK):
                 for s in range(STREAMS):
-                    on_vector = chunk == PACK - 1
                     quantise_map_chunk(
-                        nc, regroup, on_vector, x_maps[b, s], chunk, x_codes[s], x_scales[s]
+                        nc, regroup, s == 1, x_maps[b, s], chunk, x_codes[s], x_scales[s]
                     )
+            if b + 1 < BATCH:
+                quantised_softmax(b + 1)
             for j in range(PACK):
                 total = totals[j]
+                sums = {}
                 for r in range(QUARTERS):
-                    m_cols = slice(j * CHUNK + r * P, j * CHUNK + (r + 1) * P)
-                    c_cols = slice(r * C, (r + 1) * C)
-                    sums = sum_banks.tile([P, C], F32, name="sums")
-                    for s in range(STREAMS):
+                    sums[r] = sum_banks.tile([P, C], F32, name="sums")
+                for s in range(STREAMS):
+                    for r in range(QUARTERS):
+                        m_cols = slice(j * CHUNK + r * P, j * CHUNK + (r + 1) * P)
                         nc.tensor.matmul_mx(
-                            out=sums[:],
+                            out=sums[r][:],
                             lhsT=x_codes[s][:, m_cols].bitcast(FP8X4),
                             lhsT_scale=x_scales[s][:, m_cols],
-                            rhs=p_codes[s][:].bitcast(FP8X4),
-                            rhs_scale=p_scales[s][:],
+                            rhs=p_codes[b, s][:].bitcast(FP8X4),
+                            rhs_scale=p_scales[b, s][:],
                             start=(s == 0),
                             stop=(s == STREAMS - 1),
                         )
+                for r in range(QUARTERS):
+                    c_cols = slice(r * C, (r + 1) * C)
                     nc.vector.tensor_tensor(
-                        out=total[:, c_cols], in0=sums[:], in1=total[:, c_cols], op=ALU.add
+                        out=total[:, c_cols], in0=sums[r][:], in1=total[:, c_cols], op=ALU.add
                     )
                     nc.sync.dma_start(
                         out=out[b, j * P : (j + 1) * P].rearrange("m h w -> m (h w)")[:, c_cols],

@@ -21,7 +21,6 @@ N = 2048
 ROW_TILES = C // P
 QUARTERS = N // C
 CHUNK = N // PACK
-GPSIMD_QUARTERS = 2
 FOLDED = 64
 
 FLOPS = 2 * STREAMS * BATCH * C * C * N
@@ -177,21 +176,22 @@ def tile_interfusion_pb_kernel(tc, logits1, logits2, x1, x2, out):
             totals = {}
             for j in range(PACK):
                 totals[j] = results.tile([P, N], F32, name="total")
-                for r in range(GPSIMD_QUARTERS):
-                    c_cols = slice(r * C, (r + 1) * C)
-                    nc.gpsimd.tensor_tensor(
-                        out=totals[j][:, c_cols],
-                        in0=x_maps[b, 0][:, j, c_cols],
-                        in1=x_maps[b, 1][:, j, c_cols],
+                if b == 0:
+                    nc.vector.tensor_tensor(
+                        out=totals[j][:],
+                        in0=x_maps[b, 0][:, j, :],
+                        in1=x_maps[b, 1][:, j, :],
                         op=ALU.add,
                     )
-                rest = slice(GPSIMD_QUARTERS * C, N)
-                nc.vector.tensor_tensor(
-                    out=totals[j][:, rest],
-                    in0=x_maps[b, 0][:, j, rest],
-                    in1=x_maps[b, 1][:, j, rest],
-                    op=ALU.add,
-                )
+                else:
+                    for r in range(QUARTERS):
+                        c_cols = slice(r * C, (r + 1) * C)
+                        nc.gpsimd.tensor_tensor(
+                            out=totals[j][:, c_cols],
+                            in0=x_maps[b, 0][:, j, c_cols],
+                            in1=x_maps[b, 1][:, j, c_cols],
+                            op=ALU.add,
+                        )
             for chunk in range(PACK):
                 for s in range(STREAMS):
                     quantise_map_chunk(

@@ -20,96 +20,10 @@ C = 512
 N = 2048
 ROW_TILES = C // P
 QUARTERS = N // C
-CHUNK = N // PACK
+TILE = C
 FOLDED = 64
 
 FLOPS = 2 * STREAMS * BATCH * C * C * N
-
-
-def negated_row_maxima(nc, work, small, scores):
-    folded = work.tile([P, ROW_TILES, C // 2], BF16, name="folded")
-    nc.vector.tensor_tensor(
-        out=folded[:], in0=scores[:, :, : C // 2], in1=scores[:, :, C // 2 :], op=ALU.max
-    )
-    width = C // 4
-    while width >= FOLDED:
-        nc.vector.tensor_tensor(
-            out=folded[:, :, :width],
-            in0=folded[:, :, :width],
-            in1=folded[:, :, width : 2 * width],
-            op=ALU.max,
-        )
-        width //= 2
-    neg_max = small.tile([P, ROW_TILES], F32, name="neg_max")
-    nc.vector.tensor_reduce(
-        out=neg_max[:], in_=folded[:, :, :FOLDED], axis=AXIS.X, op=ALU.max, negate=True
-    )
-    return neg_max
-
-
-def softmax_rows(nc, work, small, scores, neg_max):
-    exps = work.tile([P, ROW_TILES, C], F32, name="exps")
-    row_sum = small.tile([P, ROW_TILES], F32, name="row_sum")
-    for a in range(ROW_TILES):
-        nc.scalar.activation(
-            out=exps[:, a, :],
-            in_=scores[:, a, :],
-            func=ACT.Exp,
-            bias=neg_max[:, a : a + 1],
-            scale=1.0,
-            accum_out=row_sum[:, a : a + 1],
-        )
-    inv_sum = small.tile([P, ROW_TILES], F32, name="inv_sum")
-    nc.vector.reciprocal(out=inv_sum[:], in_=row_sum[:])
-    probs = work.tile([P, ROW_TILES, C], BF16, name="probs")
-    for a in range(ROW_TILES):
-        nc.scalar.activation(
-            out=probs[:, a, :], in_=exps[:, a, :], func=ACT.Copy, scale=inv_sum[:, a : a + 1]
-        )
-    return probs
-
-
-def quantise_probs(nc, work, turn_banks, identity, probs, codes, scales):
-    grouped = work.tile([P, C, PACK], BF16, name="p_grouped", align_bytes=64)
-    for half in range(2):
-        turned = turn_banks.tile([P, 2, PACK, P], BF16, name="turned")
-        for a in range(2):
-            for t in range(PACK):
-                nc.tensor.transpose(
-                    turned[:, a, t, :],
-                    probs[:, 2 * half + a, t * P : (t + 1) * P],
-                    identity[:],
-                )
-        nc.scalar.copy(
-            out=grouped[:, 2 * half * P : 2 * (half + 1) * P, :].rearrange(
-                "q (a c) t -> q a c t", a=2
-            ),
-            in_=turned[:].rearrange("q a t c -> q a c t"),
-        )
-    nc.vector.quantize_mx(
-        out=codes.bitcast(FP8X4),
-        scales=scales,
-        in_=grouped[:].rearrange("q c t -> q (c t)"),
-    )
-
-
-def quantise_map_chunk(nc, work, on_vector, x_map, chunk, codes, scales):
-    cols = slice(chunk * CHUNK, (chunk + 1) * CHUNK)
-    grouped = work.tile(
-        [P, PACK * CHUNK],
-        BF16,
-        name="x_grouped_vector" if on_vector else "x_grouped_scalar",
-        align_bytes=64,
-    )
-    source = x_map[:, :, cols].rearrange("p t (m r) -> p m t r", r=QUARTERS)
-    target = grouped[:].rearrange("p (r m t) -> p m t r", r=QUARTERS, t=PACK)
-    if on_vector:
-        nc.vector.tensor_copy(out=target, in_=source)
-    else:
-        nc.scalar.copy(out=target, in_=source)
-    nc.vector.quantize_mx(
-        out=codes[:, cols].bitcast(FP8X4), scales=scales[:, cols], in_=grouped[:]
-    )
 
 
 def tile_interfusion_pb_kernel(tc, logits1, logits2, x1, x2, out):
@@ -119,109 +33,280 @@ def tile_interfusion_pb_kernel(tc, logits1, logits2, x1, x2, out):
     with ExitStack() as stack:
         keep = stack.enter_context(tc.tile_pool(name="keep", bufs=1))
         work = stack.enter_context(tc.tile_pool(name="work", bufs=2))
-        regroup = stack.enter_context(tc.tile_pool(name="regroup", bufs=2))
-        small = stack.enter_context(tc.tile_pool(name="small", bufs=4))
+        soft = stack.enter_context(tc.tile_pool(name="soft", bufs=1))
+        regroup = stack.enter_context(tc.tile_pool(name="regroup", bufs=4))
+        codes_pool = stack.enter_context(tc.tile_pool(name="codes_pool", bufs=4))
         results = stack.enter_context(tc.tile_pool(name="results", bufs=6))
         turn_banks = stack.enter_context(tc.psum_pool(name="turn_banks", bufs=2))
-        sum_banks = stack.enter_context(tc.psum_pool(name="sum_banks", bufs=6))
+        sum_banks = stack.enter_context(tc.psum_pool(name="sum_banks", bufs=8-2))
+        stack.enter_context(tc.manual_schedule())
+
+        identity = keep.tile([P, P], F32, name="identity")
+        make_identity(nc, identity[:])
+        identity16 = keep.tile([P, P], BF16, name="identity16")
+        make_identity(nc, identity16[:])
+        warm = keep.tile([P, 1], F32, name="warm")
+        nc.gpsimd.memset(warm[:], 0.0)
+        nc.scalar.activation(out=warm[:], in_=warm[:], func=ACT.Exp)
 
         scores = {}
         x_maps = {}
-        for b in range(BATCH):
+        neg_max = {}
+        exps = {}
+        row_sum = {}
+        inv_sum = {}
+        probs = {}
+        p_grouped = {}
+        p_codes = {}
+        p_scales = {}
+        grouped = {}
+        x_codes = {}
+        x_scales = {}
+        totals = {}
+        sums = {}
+
+        def load_scores(b):
             for s in range(STREAMS):
                 scores[b, s] = keep.tile([P, ROW_TILES, C], BF16, name="scores_%d_%d" % (b, s))
                 nc.sync.dma_start(
                     out=scores[b, s][:], in_=logits[s][b].rearrange("(a p) k -> p a k", p=P)
                 )
+
+        def load_plane(b, t):
             for s in range(STREAMS):
-                x_maps[b, s] = keep.tile([P, PACK, N], BF16, name="x_map_%d_%d" % (b, s))
-            for t in range(PACK):
-                for s in range(STREAMS):
-                    nc.sync.dma_start(
-                        out=x_maps[b, s][:, t, :],
-                        in_=maps[s][b, t * P : (t + 1) * P].rearrange("p h w -> p (h w)"),
-                    )
-
-        identity = keep.tile([P, P], BF16, name="identity")
-        make_identity(nc, identity[:])
-
-        p_codes = {}
-        p_scales = {}
-
-        neg_maxima = {}
-
-        def row_maxima(b):
-            for s in range(STREAMS):
-                neg_maxima[b, s] = negated_row_maxima(nc, work, small, scores[b, s])
-
-        def quantised_softmax(b):
-            for s in range(STREAMS):
-                p_codes[b, s] = work.tile([P, C], U32, name="p_codes_%d" % s, align_bytes=64)
-                p_scales[b, s] = work.tile([P, C], U8, name="p_scales_%d" % s, align_bytes=64)
-                probs = softmax_rows(nc, work, small, scores[b, s], neg_maxima[b, s])
-                quantise_probs(
-                    nc, work, turn_banks, identity, probs, p_codes[b, s][:], p_scales[b, s][:]
+                if t == 0:
+                    x_maps[b, s] = keep.tile([P, PACK, N], BF16, name="x_map_%d_%d" % (b, s))
+                nc.sync.dma_start(
+                    out=x_maps[b, s][:, t, :],
+                    in_=maps[s][b].rearrange("(p t) h w -> p t (h w)", t=PACK)[:, t, :],
                 )
 
-        row_maxima(0)
-        quantised_softmax(0)
-        for b in range(BATCH):
-            if b + 1 < BATCH:
-                row_maxima(b + 1)
-            x_codes = {}
-            x_scales = {}
-            for s in range(STREAMS):
-                x_codes[s] = work.tile([P, N], U32, name="x_codes_%d" % s, align_bytes=64)
-                x_scales[s] = work.tile([P, N], U8, name="x_scales_%d" % s, align_bytes=64)
-            totals = {}
-            for j in range(PACK):
-                totals[j] = results.tile([P, N], F32, name="total")
-                if b == 0:
+        def row_maxima(b, streams):
+            folded = {}
+            for s in streams:
+                folded[s] = soft.tile([P, ROW_TILES, C // 2], BF16, name="folded_%d" % s)
+                nc.vector.tensor_tensor(
+                    out=folded[s][:], in0=scores[b, s][:, :, : C // 2], in1=scores[b, s][:, :, C // 2 :], op=ALU.max
+                )
+            width = C // 4
+            while width >= FOLDED:
+                for s in streams:
                     nc.vector.tensor_tensor(
-                        out=totals[j][:],
-                        in0=x_maps[b, 0][:, j, :],
-                        in1=x_maps[b, 1][:, j, :],
-                        op=ALU.add,
+                        out=folded[s][:, :, :width],
+                        in0=folded[s][:, :, :width],
+                        in1=folded[s][:, :, width : 2 * width],
+                        op=ALU.max,
                     )
-                else:
-                    for r in range(QUARTERS):
-                        c_cols = slice(r * C, (r + 1) * C)
-                        nc.gpsimd.tensor_tensor(
-                            out=totals[j][:, c_cols],
-                            in0=x_maps[b, 0][:, j, c_cols],
-                            in1=x_maps[b, 1][:, j, c_cols],
-                            op=ALU.add,
-                        )
-            for chunk in range(PACK):
+                width //= 2
+            for s in streams:
+                neg_max[b, s] = keep.tile([P, ROW_TILES], F32, name="neg_max_%d_%d" % (b, s))
+                nc.vector.tensor_reduce(
+                    out=neg_max[b, s][:], in_=folded[s][:, :, :FOLDED], axis=AXIS.X, op=ALU.max, negate=True
+                )
+
+        def exponentials(b, s):
+            exps[b, s] = soft.tile([P, ROW_TILES, C], F32, name="exps_%d" % s)
+            row_sum[b, s] = keep.tile([P, ROW_TILES], F32, name="row_sum_%d_%d" % (b, s))
+            for a in range(ROW_TILES):
+                nc.scalar.activation(
+                    out=exps[b, s][:, a, :],
+                    in_=scores[b, s][:, a, :],
+                    func=ACT.Exp,
+                    bias=neg_max[b, s][:, a : a + 1],
+                    scale=1.0,
+                    accum_out=row_sum[b, s][:, a : a + 1],
+                )
+
+        def reciprocals(b, s):
+            inv_sum[b, s] = keep.tile([P, ROW_TILES], F32, name="inv_sum_%d_%d" % (b, s))
+            nc.vector.reciprocal(out=inv_sum[b, s][:], in_=row_sum[b, s][:])
+
+        def normalise(b, s):
+            probs[b, s] = soft.tile([P, ROW_TILES, C], BF16, name="probs_%d" % s)
+            for a in range(ROW_TILES):
+                nc.scalar.activation(
+                    out=probs[b, s][:, a, :],
+                    in_=exps[b, s][:, a, :],
+                    func=ACT.Copy,
+                    scale=inv_sum[b, s][:, a : a + 1],
+                )
+
+        def turn(b, s):
+            p_grouped[b, s] = soft.tile([P, C, PACK], BF16, name="p_grouped_%d" % s, align_bytes=64)
+            for half in range(2):
+                turned = turn_banks.tile([P, 2, 2, P], F32, name="turned")
+                for a in range(2):
+                    words = probs[b, s][:, 2 * half + a, :].bitcast(F32)
+                    for u in range(2):
+                        nc.tensor.transpose(turned[:, u, a, :], words[:, u::2], identity[:])
+                nc.scalar.copy(
+                    out=p_grouped[b, s][:, 2 * half * P : 2 * (half + 1) * P, :].rearrange("p c t -> p (c t)").bitcast(F32).rearrange("p (c u) -> p c u", u=2),
+                    in_=turned[:].rearrange("p u a c -> p (a c) u"),
+                )
+
+        def quantise_p(b, s):
+            p_codes[b, s] = work.tile([P, C], U32, name="p_codes_%d" % s, align_bytes=64)
+            p_scales[b, s] = work.tile([P, C], U8, name="p_scales_%d" % s, align_bytes=64)
+            nc.vector.quantize_mx(
+                out=p_codes[b, s][:].bitcast(FP8X4), scales=p_scales[b, s][:], in_=p_grouped[b, s][:].rearrange("p c t -> p (c t)")
+            )
+
+        def group_pe(b, s, j):
+            grouped[b, s, j] = regroup.tile([P, PACK * TILE], BF16, name="grouped_scalar", align_bytes=64)
+            source = x_maps[b, s][:].rearrange("p t (m q r) -> p q t m r", q=PACK, r=QUARTERS)[:, j]
+            for i in range(2):
+                bank = turn_banks.tile([P, TILE // 2 * PACK], BF16, name="turned")
+                spread = bank[:].rearrange("p (r m t) -> p t m r", r=2, t=PACK)
+                for t in range(PACK):
+                    nc.tensor.matmul(
+                        out=spread[:, t], lhsT=identity16[:], rhs=source[:, t, :, 2 * i : 2 * i + 2], start=True, stop=True
+                    )
+                half = slice(i * TILE // 2 * PACK, (i + 1) * TILE // 2 * PACK)
+                nc.scalar.copy(out=grouped[b, s, j][:, half], in_=bank[:])
+
+        def group(b, s, j, on_vector):
+            grouped[b, s, j] = regroup.tile(
+                [P, PACK * TILE], BF16, name="grouped_vector" if on_vector else "grouped_scalar", align_bytes=64
+            )
+            source = x_maps[b, s][:].rearrange("p t (m q r) -> p q m t r", q=PACK, r=QUARTERS)[:, j]
+            target = grouped[b, s, j][:].rearrange("p (r m t) -> p m t r", r=QUARTERS, t=PACK)
+            if on_vector:
+                nc.vector.tensor_copy(out=target, in_=source)
+            else:
+                nc.scalar.copy(out=target, in_=source)
+
+        def quantise_x(b, s, j):
+            x_codes[b, s, j] = codes_pool.tile([P, TILE], U32, name="x_codes_%d" % s, align_bytes=64)
+            x_scales[b, s, j] = codes_pool.tile([P, TILE], U8, name="x_scales_%d" % s, align_bytes=64)
+            nc.vector.quantize_mx(
+                out=x_codes[b, s, j][:].bitcast(FP8X4), scales=x_scales[b, s, j][:], in_=grouped[b, s, j][:]
+            )
+
+        def residual(b, j, parts=1):
+            totals[b, j] = results.tile([P, N], F32, name="total")
+            for i in range(parts):
+                cols = slice(i * N // parts, (i + 1) * N // parts)
+                nc.vector.tensor_tensor(
+                    out=totals[b, j][:, cols], in0=x_maps[b, 0][:, j, cols], in1=x_maps[b, 1][:, j, cols], op=ALU.add
+                )
+
+        def open_residual(b, j):
+            totals[b, j] = results.tile([P, N], F32, name="total")
+
+        def residual_part(b, j, parts):
+            for i in parts:
+                cols = slice(i * C, (i + 1) * C)
+                nc.vector.tensor_tensor(
+                    out=totals[b, j][:, cols], in0=x_maps[b, 0][:, j, cols], in1=x_maps[b, 1][:, j, cols], op=ALU.add
+                )
+
+        def residual_g(b, j, parts):
+            for i in parts:
+                nc.vector.memset(totals[b, j][:, i * C : i * C + 1], 0.0)
+                cols = slice(i * C, (i + 1) * C)
+                nc.gpsimd.tensor_tensor(
+                    out=totals[b, j][:, cols], in0=x_maps[b, 0][:, j, cols], in1=x_maps[b, 1][:, j, cols], op=ALU.add
+                )
+
+        def multiply(b, j):
+            for r in range(QUARTERS):
+                sums[b, j, r] = sum_banks.tile([P, C], F32, name="sums")
+            for r in range(QUARTERS):
                 for s in range(STREAMS):
-                    quantise_map_chunk(
-                        nc, regroup, s == 1, x_maps[b, s], chunk, x_codes[s], x_scales[s]
+                    m_cols = slice(r * P, (r + 1) * P)
+                    nc.tensor.matmul_mx(
+                        out=sums[b, j, r][:],
+                        lhsT=x_codes[b, s, j][:, m_cols].bitcast(FP8X4),
+                        lhsT_scale=x_scales[b, s, j][:, m_cols],
+                        rhs=p_codes[b, s][:].bitcast(FP8X4),
+                        rhs_scale=p_scales[b, s][:],
+                        start=(s == 0),
+                        stop=(s == STREAMS - 1),
                     )
-            if b + 1 < BATCH:
-                quantised_softmax(b + 1)
-            for j in range(PACK):
-                total = totals[j]
-                sums = {}
-                for r in range(QUARTERS):
-                    sums[r] = sum_banks.tile([P, C], F32, name="sums")
+
+        def finish(b, j):
+            for r in range(QUARTERS):
+                cols = slice(r * C, (r + 1) * C)
+                nc.vector.tensor_tensor(
+                    out=totals[b, j][:, cols], in0=sums[b, j, r][:], in1=totals[b, j][:, cols], op=ALU.add
+                )
+                nc.sync.dma_start(
+                    out=out[b].rearrange("(p t) h w -> p t (h w)", t=PACK)[:, j, cols], in_=totals[b, j][:, cols]
+                )
+
+        load_scores(0)
+        load_plane(0, 0)
+        load_plane(0, 1)
+        load_scores(1)
+        for t in range(2, 4):
+            load_plane(0, t)
+        for t in range(4):
+            load_plane(1, t)
+        row_maxima(0, [0])
+        row_maxima(0, [1])
+        exponentials(0, 0)
+        exponentials(0, 1)
+        residual(0, 0)
+        reciprocals(0, 0)
+        normalise(0, 0)
+        turn(0, 0)
+        residual(0, 1)
+        reciprocals(0, 1)
+        normalise(0, 1)
+        turn(0, 1)
+        row_maxima(1, [0, 1])
+        residual(0, 2)
+        residual(0, 3)
+
+        PE_CHUNKS = ()
+        V_CHUNKS = ((0, 1, 0), (0, 1, 1), (0, 1, 2), (0, 1, 3), (1, 1, 3))
+        def regroup_tile(i):
+            if i < 8:
+                b, j = divmod(i, 4)
+                for s in (1, 0):
+                    if (b, s, j) in PE_CHUNKS:
+                        group_pe(b, s, j)
+                    else:
+                        group(b, s, j, (b, s, j) in V_CHUNKS)
+        def quantise_tile(i):
+            if i < 8:
+                b, j = divmod(i, 4)
                 for s in range(STREAMS):
-                    for r in range(QUARTERS):
-                        m_cols = slice(j * CHUNK + r * P, j * CHUNK + (r + 1) * P)
-                        nc.tensor.matmul_mx(
-                            out=sums[r][:],
-                            lhsT=x_codes[s][:, m_cols].bitcast(FP8X4),
-                            lhsT_scale=x_scales[s][:, m_cols],
-                            rhs=p_codes[b, s][:].bitcast(FP8X4),
-                            rhs_scale=p_scales[b, s][:],
-                            start=(s == 0),
-                            stop=(s == STREAMS - 1),
-                        )
-                for r in range(QUARTERS):
-                    c_cols = slice(r * C, (r + 1) * C)
-                    nc.vector.tensor_tensor(
-                        out=total[:, c_cols], in0=sums[r][:], in1=total[:, c_cols], op=ALU.add
-                    )
-                    nc.sync.dma_start(
-                        out=out[b, j * P : (j + 1) * P].rearrange("m h w -> m (h w)")[:, c_cols],
-                        in_=total[:, c_cols],
-                    )
+                    quantise_x(b, s, j)
+        def g_part(j):
+            if False:
+                if j % 2 == 0:
+                    open_residual(1, j // 2)
+                residual_g(1, j // 2, (0, 1) if j % 2 == 0 else (2, 3))
+        regroup_tile(0)
+        quantise_p(0, 0)
+        quantise_p(0, 1)
+        regroup_tile(1)
+        quantise_tile(0)
+        multiply(0, 0)
+        for i in range(8):
+            b, j = divmod(i, 4)
+            if i == 0:
+                exponentials(1, 0)
+                exponentials(1, 1)
+            if i == 1:
+                normalise(1, 0)
+            if i == 2:
+                normalise(1, 1)
+                turn(1, 0)
+                turn(1, 1)
+            regroup_tile(i + 2)
+            if i == 3:
+                quantise_p(1, 0)
+                quantise_p(1, 1)
+            quantise_tile(i + 1)
+            if i + 1 < 8:
+                multiply(*divmod(i + 1, 4))
+            if i < 4 and (i >= 2 or not False):
+                residual(1, i)
+            if i == 0:
+                reciprocals(1, 0)
+                reciprocals(1, 1)
+            if i < 4:
+                g_part(i)
+            finish(b, j)

@@ -38,7 +38,7 @@ def tile_interfusion_pb_kernel(tc, logits1, logits2, x1, x2, out):
         codes_pool = stack.enter_context(tc.tile_pool(name="codes_pool", bufs=4))
         results = stack.enter_context(tc.tile_pool(name="results", bufs=6))
         turn_banks = stack.enter_context(tc.psum_pool(name="turn_banks", bufs=2))
-        sum_banks = stack.enter_context(tc.psum_pool(name="sum_banks", bufs=8-2))
+        sum_banks = stack.enter_context(tc.psum_pool(name="sum_banks", bufs=6))
         stack.enter_context(tc.manual_schedule())
 
         identity = keep.tile([P, P], F32, name="identity")
@@ -153,16 +153,21 @@ def tile_interfusion_pb_kernel(tc, logits1, logits2, x1, x2, out):
 
         def group_pe(b, s, j):
             grouped[b, s, j] = regroup.tile([P, PACK * TILE], BF16, name="grouped_scalar", align_bytes=64)
-            source = x_maps[b, s][:].rearrange("p t (m q r) -> p q t m r", q=PACK, r=QUARTERS)[:, j]
+            source = x_maps[b, s][:].rearrange("p t (m q r) -> p q m r t", q=PACK, r=QUARTERS)[:, j]
+            target = grouped[b, s, j][:].rearrange("p (r m t) -> p r m t", r=QUARTERS, t=PACK)
             for i in range(2):
-                bank = turn_banks.tile([P, TILE // 2 * PACK], BF16, name="turned")
-                spread = bank[:].rearrange("p (r m t) -> p t m r", r=2, t=PACK)
-                for t in range(PACK):
+                bank = turn_banks.tile([P, QUARTERS, P // 2, PACK], BF16, name="spread")
+                spread = bank[:].rearrange("p r m t -> p m r t")
+                for h in range(2):
+                    m0 = i * P // 2 + h * P // 4
                     nc.tensor.matmul(
-                        out=spread[:, t], lhsT=identity16[:], rhs=source[:, t, :, 2 * i : 2 * i + 2], start=True, stop=True
+                        out=spread[:, h * P // 4 : (h + 1) * P // 4],
+                        lhsT=identity16[:],
+                        rhs=source[:, m0 : m0 + P // 4],
+                        start=True,
+                        stop=True,
                     )
-                half = slice(i * TILE // 2 * PACK, (i + 1) * TILE // 2 * PACK)
-                nc.scalar.copy(out=grouped[b, s, j][:, half], in_=bank[:])
+                nc.scalar.copy(out=target[:, :, i * P // 2 : (i + 1) * P // 2], in_=bank[:])
 
         def group(b, s, j, on_vector):
             grouped[b, s, j] = regroup.tile(
@@ -201,12 +206,11 @@ def tile_interfusion_pb_kernel(tc, logits1, logits2, x1, x2, out):
                 )
 
         def residual_g(b, j, parts):
-            for i in parts:
-                nc.vector.memset(totals[b, j][:, i * C : i * C + 1], 0.0)
-                cols = slice(i * C, (i + 1) * C)
-                nc.gpsimd.tensor_tensor(
-                    out=totals[b, j][:, cols], in0=x_maps[b, 0][:, j, cols], in1=x_maps[b, 1][:, j, cols], op=ALU.add
-                )
+            cols = slice(parts[0] * C, (parts[-1] + 1) * C)
+            nc.vector.memset(totals[b, j][:, parts[0] * C : parts[0] * C + 1], 0.0)
+            nc.gpsimd.tensor_tensor(
+                out=totals[b, j][:, cols], in0=x_maps[b, 0][:, j, cols], in1=x_maps[b, 1][:, j, cols], op=ALU.add
+            )
 
         def multiply(b, j):
             for r in range(QUARTERS):
@@ -259,7 +263,9 @@ def tile_interfusion_pb_kernel(tc, logits1, logits2, x1, x2, out):
         residual(0, 3)
 
         PE_CHUNKS = ()
-        V_CHUNKS = ((0, 1, 0), (0, 1, 1), (0, 1, 2), (0, 1, 3), (1, 1, 3))
+        V_CHUNKS = ((0, 1, 0), (0, 1, 1), (0, 1, 2), (0, 1, 3), (1, 1, 1), (1, 1, 3))
+        G_WINDOWS = {0: (4, (0, 1)), 1: (4, (2, 3)), 2: (5, (0, 1)), 3: (5, (2, 3)), 4: (6, (0, 1)), 5: (6, (2, 3))}
+        V_RESIDUALS = {3: (7, (0, 1, 2, 3))}
         def regroup_tile(i):
             if i < 8:
                 b, j = divmod(i, 4)
@@ -273,11 +279,18 @@ def tile_interfusion_pb_kernel(tc, logits1, logits2, x1, x2, out):
                 b, j = divmod(i, 4)
                 for s in range(STREAMS):
                     quantise_x(b, s, j)
-        def g_part(j):
-            if False:
-                if j % 2 == 0:
-                    open_residual(1, j // 2)
-                residual_g(1, j // 2, (0, 1) if j % 2 == 0 else (2, 3))
+        def g_part(i):
+            if i in G_WINDOWS:
+                tile, parts = G_WINDOWS[i]
+                if divmod(tile, 4) not in totals:
+                    open_residual(*divmod(tile, 4))
+                residual_g(*divmod(tile, 4), parts)
+        def v_part(i):
+            if i in V_RESIDUALS:
+                tile, parts = V_RESIDUALS[i]
+                if divmod(tile, 4) not in totals:
+                    open_residual(*divmod(tile, 4))
+                residual_part(*divmod(tile, 4), parts)
         regroup_tile(0)
         quantise_p(0, 0)
         quantise_p(0, 1)
@@ -296,17 +309,15 @@ def tile_interfusion_pb_kernel(tc, logits1, logits2, x1, x2, out):
                 turn(1, 0)
                 turn(1, 1)
             regroup_tile(i + 2)
+            v_part(i)
             if i == 3:
                 quantise_p(1, 0)
                 quantise_p(1, 1)
             quantise_tile(i + 1)
             if i + 1 < 8:
                 multiply(*divmod(i + 1, 4))
-            if i < 4 and (i >= 2 or not False):
-                residual(1, i)
             if i == 0:
                 reciprocals(1, 0)
                 reciprocals(1, 1)
-            if i < 4:
-                g_part(i)
+            g_part(i)
             finish(b, j)

@@ -38,7 +38,7 @@ def tile_interfusion_pb_kernel(tc, logits1, logits2, x1, x2, out):
         codes_pool = stack.enter_context(tc.tile_pool(name="codes_pool", bufs=4))
         results = stack.enter_context(tc.tile_pool(name="results", bufs=6))
         turn_banks = stack.enter_context(tc.psum_pool(name="turn_banks", bufs=2))
-        sum_banks = stack.enter_context(tc.psum_pool(name="sum_banks", bufs=6))
+        sum_banks = stack.enter_context(tc.psum_pool(name="sum_banks", bufs=4))
         stack.enter_context(tc.manual_schedule())
 
         identity = keep.tile([P, P], F32, name="identity")
@@ -68,9 +68,11 @@ def tile_interfusion_pb_kernel(tc, logits1, logits2, x1, x2, out):
         def load_scores(b):
             for s in range(STREAMS):
                 scores[b, s] = keep.tile([P, ROW_TILES, C], BF16, name="scores_%d_%d" % (b, s))
-                nc.sync.dma_start(
-                    out=scores[b, s][:], in_=logits[s][b].rearrange("(a p) k -> p a k", p=P)
-                )
+                view = logits[s][b].rearrange("(a p) k -> p a k", p=P)
+                pieces = 2 if b == 0 else 1
+                for h in range(pieces):
+                    rows = slice(h * ROW_TILES // pieces, (h + 1) * ROW_TILES // pieces)
+                    nc.sync.dma_start(out=scores[b, s][:, rows], in_=view[:, rows])
 
         def load_plane(b, t):
             for s in range(STREAMS):
@@ -81,27 +83,31 @@ def tile_interfusion_pb_kernel(tc, logits1, logits2, x1, x2, out):
                     in_=maps[s][b].rearrange("(p t) h w -> p t (h w)", t=PACK)[:, t, :],
                 )
 
-        def row_maxima(b, streams):
+        def row_maxima(b, pieces):
             folded = {}
-            for s in streams:
-                folded[s] = soft.tile([P, ROW_TILES, C // 2], BF16, name="folded_%d" % s)
+            for s, a, n in pieces:
+                if a == 0:
+                    neg_max[b, s] = keep.tile([P, ROW_TILES], F32, name="neg_max_%d_%d" % (b, s))
+                folded[s, a] = soft.tile([P, n, C // 2], BF16, name="folded_%d_%d_%d" % (b, s, a))
                 nc.vector.tensor_tensor(
-                    out=folded[s][:], in0=scores[b, s][:, :, : C // 2], in1=scores[b, s][:, :, C // 2 :], op=ALU.max
+                    out=folded[s, a][:],
+                    in0=scores[b, s][:, a : a + n, : C // 2],
+                    in1=scores[b, s][:, a : a + n, C // 2 :],
+                    op=ALU.max,
                 )
             width = C // 4
             while width >= FOLDED:
-                for s in streams:
+                for s, a, n in pieces:
                     nc.vector.tensor_tensor(
-                        out=folded[s][:, :, :width],
-                        in0=folded[s][:, :, :width],
-                        in1=folded[s][:, :, width : 2 * width],
+                        out=folded[s, a][:, :, :width],
+                        in0=folded[s, a][:, :, :width],
+                        in1=folded[s, a][:, :, width : 2 * width],
                         op=ALU.max,
                     )
                 width //= 2
-            for s in streams:
-                neg_max[b, s] = keep.tile([P, ROW_TILES], F32, name="neg_max_%d_%d" % (b, s))
+            for s, a, n in pieces:
                 nc.vector.tensor_reduce(
-                    out=neg_max[b, s][:], in_=folded[s][:, :, :FOLDED], axis=AXIS.X, op=ALU.max, negate=True
+                    out=neg_max[b, s][:, a : a + n], in_=folded[s, a][:, :, :FOLDED], axis=AXIS.X, op=ALU.max, negate=True
                 )
 
         def exponentials(b, s):
@@ -153,11 +159,11 @@ def tile_interfusion_pb_kernel(tc, logits1, logits2, x1, x2, out):
 
         def group_pe(b, s, j):
             grouped[b, s, j] = regroup.tile([P, PACK * TILE], BF16, name="grouped_scalar", align_bytes=64)
-            source = x_maps[b, s][:].rearrange("p t (m q r) -> p q m r t", q=PACK, r=QUARTERS)[:, j]
+            source = x_maps[b, s][:].rearrange("p t (m q r) -> p q m t r", q=PACK, r=QUARTERS)[:, j]
             target = grouped[b, s, j][:].rearrange("p (r m t) -> p r m t", r=QUARTERS, t=PACK)
             for i in range(2):
                 bank = turn_banks.tile([P, QUARTERS, P // 2, PACK], BF16, name="spread")
-                spread = bank[:].rearrange("p r m t -> p m r t")
+                spread = bank[:].rearrange("p r m t -> p m t r")
                 for h in range(2):
                     m0 = i * P // 2 + h * P // 4
                     nc.tensor.matmul(
@@ -246,8 +252,8 @@ def tile_interfusion_pb_kernel(tc, logits1, logits2, x1, x2, out):
             load_plane(0, t)
         for t in range(4):
             load_plane(1, t)
-        row_maxima(0, [0])
-        row_maxima(0, [1])
+        row_maxima(0, [(0, 0, 2), (0, 2, 2)])
+        row_maxima(0, [(1, 0, 2), (1, 2, 2)])
         exponentials(0, 0)
         exponentials(0, 1)
         residual(0, 0)
@@ -258,14 +264,13 @@ def tile_interfusion_pb_kernel(tc, logits1, logits2, x1, x2, out):
         reciprocals(0, 1)
         normalise(0, 1)
         turn(0, 1)
-        row_maxima(1, [0, 1])
+        row_maxima(1, [(0, 0, 4), (1, 0, 4)])
         residual(0, 2)
         residual(0, 3)
-
-        PE_CHUNKS = ()
-        V_CHUNKS = ((0, 1, 0), (0, 1, 1), (0, 1, 2), (0, 1, 3), (1, 1, 1), (1, 1, 3))
-        G_WINDOWS = {0: (4, (0, 1)), 1: (4, (2, 3)), 2: (5, (0, 1)), 3: (5, (2, 3)), 4: (6, (0, 1)), 5: (6, (2, 3))}
-        V_RESIDUALS = {3: (7, (0, 1, 2, 3))}
+        PE_CHUNKS = ((0, 0, 1), (0, 0, 3), (1, 0, 0), (1, 0, 1), (1, 0, 2), (1, 0, 3))
+        V_CHUNKS = ((0, 1, 0), (0, 1, 1), (0, 1, 2), (0, 1, 3), (1, 1, 3))
+        G_WINDOWS = {0: (4, (0, 1)), 1: (4, (2, 3)), 2: (5, (0, 1)), 3: (5, (2, 3)), 4: (6, (0, 1)), 5: (6, (2, 3)), 6: (7, (2, 3))}
+        V_RESIDUALS = {3: (7, (0, 1))}
         def regroup_tile(i):
             if i < 8:
                 b, j = divmod(i, 4)

@@ -64,6 +64,8 @@ def tile_interfusion_pb_kernel(tc, logits1, logits2, x1, x2, out):
         x_scales = {}
         totals = {}
         sums = {}
+        banks = {}
+        folded = {}
 
         def load_scores(b):
             for s in range(STREAMS):
@@ -83,32 +85,34 @@ def tile_interfusion_pb_kernel(tc, logits1, logits2, x1, x2, out):
                     in_=maps[s][b].rearrange("(p t) h w -> p t (h w)", t=PACK)[:, t, :],
                 )
 
-        def row_maxima(b, pieces):
-            folded = {}
-            for s, a, n in pieces:
-                if a == 0:
-                    neg_max[b, s] = keep.tile([P, ROW_TILES], F32, name="neg_max_%d_%d" % (b, s))
+        def fold(b, s, a, n, width):
+            first = width == C // 2
+            if first:
                 folded[s, a] = soft.tile([P, n, C // 2], BF16, name="folded_%d_%d_%d" % (b, s, a))
-                nc.vector.tensor_tensor(
-                    out=folded[s, a][:],
-                    in0=scores[b, s][:, a : a + n, : C // 2],
-                    in1=scores[b, s][:, a : a + n, C // 2 :],
-                    op=ALU.max,
-                )
-            width = C // 4
-            while width >= FOLDED:
-                for s, a, n in pieces:
-                    nc.vector.tensor_tensor(
-                        out=folded[s, a][:, :, :width],
-                        in0=folded[s, a][:, :, :width],
-                        in1=folded[s, a][:, :, width : 2 * width],
-                        op=ALU.max,
-                    )
-                width //= 2
-            for s, a, n in pieces:
-                nc.vector.tensor_reduce(
-                    out=neg_max[b, s][:, a : a + n], in_=folded[s, a][:, :, :FOLDED], axis=AXIS.X, op=ALU.max, negate=True
-                )
+            source = scores[b, s][:, a : a + n] if first else folded[s, a][:]
+            nc.vector.tensor_tensor(
+                out=folded[s, a][:, :, :width],
+                in0=source[:, :, :width],
+                in1=source[:, :, width : 2 * width],
+                op=ALU.max,
+            )
+
+        def reduce_folded(b, s, a, n):
+            if (b, s) not in neg_max:
+                neg_max[b, s] = keep.tile([P, ROW_TILES], F32, name="neg_max_%d_%d" % (b, s))
+            nc.vector.tensor_reduce(
+                out=neg_max[b, s][:, a : a + n], in_=folded[s, a][:, :, :FOLDED], axis=AXIS.X, op=ALU.max, negate=True
+            )
+
+        def row_maxima(b, pieces, lag=0):
+            widths = (C // 2, C // 4, C // 8)
+            for step in range(len(widths) + 1 + lag * (len(pieces) - 1)):
+                for k, (s, a, n) in enumerate(pieces):
+                    at = step - lag * k
+                    if 0 <= at < len(widths):
+                        fold(b, s, a, n, widths[at])
+                    elif at == len(widths):
+                        reduce_folded(b, s, a, n)
 
         def exponentials(b, s):
             exps[b, s] = soft.tile([P, ROW_TILES, C], F32, name="exps_%d" % s)
@@ -157,23 +161,26 @@ def tile_interfusion_pb_kernel(tc, logits1, logits2, x1, x2, out):
                 out=p_codes[b, s][:].bitcast(FP8X4), scales=p_scales[b, s][:], in_=p_grouped[b, s][:].rearrange("p c t -> p (c t)")
             )
 
-        def group_pe(b, s, j):
-            grouped[b, s, j] = regroup.tile([P, PACK * TILE], BF16, name="grouped_scalar", align_bytes=64)
+        def spread(b, s, j):
             source = x_maps[b, s][:].rearrange("p t (m q r) -> p q m t r", q=PACK, r=QUARTERS)[:, j]
-            target = grouped[b, s, j][:].rearrange("p (r m t) -> p r m t", r=QUARTERS, t=PACK)
             for i in range(2):
-                bank = turn_banks.tile([P, QUARTERS, P // 2, PACK], BF16, name="spread")
-                spread = bank[:].rearrange("p r m t -> p m t r")
+                banks[b, s, j, i] = turn_banks.tile([P, QUARTERS, P // 2, PACK], BF16, name="spread")
+                view = banks[b, s, j, i][:].rearrange("p r m t -> p m t r")
                 for h in range(2):
                     m0 = i * P // 2 + h * P // 4
                     nc.tensor.matmul(
-                        out=spread[:, h * P // 4 : (h + 1) * P // 4],
+                        out=view[:, h * P // 4 : (h + 1) * P // 4],
                         lhsT=identity16[:],
                         rhs=source[:, m0 : m0 + P // 4],
                         start=True,
                         stop=True,
                     )
-                nc.scalar.copy(out=target[:, :, i * P // 2 : (i + 1) * P // 2], in_=bank[:])
+
+        def group_pe(b, s, j):
+            grouped[b, s, j] = regroup.tile([P, PACK * TILE], BF16, name="grouped_scalar", align_bytes=64)
+            target = grouped[b, s, j][:].rearrange("p (r m t) -> p r m t", r=QUARTERS, t=PACK)
+            for i in range(2):
+                nc.scalar.copy(out=target[:, :, i * P // 2 : (i + 1) * P // 2], in_=banks[b, s, j, i][:])
 
         def group(b, s, j, on_vector):
             grouped[b, s, j] = regroup.tile(
@@ -211,9 +218,11 @@ def tile_interfusion_pb_kernel(tc, logits1, logits2, x1, x2, out):
                     out=totals[b, j][:, cols], in0=x_maps[b, 0][:, j, cols], in1=x_maps[b, 1][:, j, cols], op=ALU.add
                 )
 
+        def token(b, j, parts):
+            nc.vector.memset(totals[b, j][:, parts[0] * C : parts[0] * C + 1], 0.0)
+
         def residual_g(b, j, parts):
             cols = slice(parts[0] * C, (parts[-1] + 1) * C)
-            nc.vector.memset(totals[b, j][:, parts[0] * C : parts[0] * C + 1], 0.0)
             nc.gpsimd.tensor_tensor(
                 out=totals[b, j][:, cols], in0=x_maps[b, 0][:, j, cols], in1=x_maps[b, 1][:, j, cols], op=ALU.add
             )
@@ -252,8 +261,8 @@ def tile_interfusion_pb_kernel(tc, logits1, logits2, x1, x2, out):
             load_plane(0, t)
         for t in range(4):
             load_plane(1, t)
-        row_maxima(0, [(0, 0, 2), (0, 2, 2)])
-        row_maxima(0, [(1, 0, 2), (1, 2, 2)])
+        row_maxima(0, [(0, 0, 2), (0, 2, 2)], 1)
+        row_maxima(0, [(1, 0, 2), (1, 2, 2)], 0)
         exponentials(0, 0)
         exponentials(0, 1)
         residual(0, 0)
@@ -267,8 +276,9 @@ def tile_interfusion_pb_kernel(tc, logits1, logits2, x1, x2, out):
         row_maxima(1, [(0, 0, 4), (1, 0, 4)])
         residual(0, 2)
         residual(0, 3)
-        PE_CHUNKS = ((0, 0, 1), (0, 0, 3), (1, 0, 0), (1, 0, 1), (1, 0, 2), (1, 0, 3))
-        V_CHUNKS = ((0, 1, 0), (0, 1, 1), (0, 1, 2), (0, 1, 3), (1, 1, 3))
+
+        PE_CHUNKS = ((0, 0, 1), (0, 0, 2), (0, 0, 3), (1, 0, 0), (1, 0, 1), (1, 0, 2))
+        V_CHUNKS = ((0, 1, 0), (0, 1, 1), (0, 1, 2), (0, 1, 3), (1, 1, 0))
         G_WINDOWS = {0: (4, (0, 1)), 1: (4, (2, 3)), 2: (5, (0, 1)), 3: (5, (2, 3)), 4: (6, (0, 1)), 5: (6, (2, 3)), 6: (7, (2, 3))}
         V_RESIDUALS = {3: (7, (0, 1))}
         def regroup_tile(i):
@@ -277,18 +287,20 @@ def tile_interfusion_pb_kernel(tc, logits1, logits2, x1, x2, out):
                 for s in (1, 0):
                     if (b, s, j) in PE_CHUNKS:
                         group_pe(b, s, j)
+                        k = PE_CHUNKS.index((b, s, j)) + 1
+                        if k < len(PE_CHUNKS):
+                            spread(*PE_CHUNKS[k])
                     else:
                         group(b, s, j, (b, s, j) in V_CHUNKS)
-        def quantise_tile(i):
-            if i < 8:
-                b, j = divmod(i, 4)
-                for s in range(STREAMS):
-                    quantise_x(b, s, j)
-        def g_part(i):
+        def g_token(i):
             if i in G_WINDOWS:
                 tile, parts = G_WINDOWS[i]
                 if divmod(tile, 4) not in totals:
                     open_residual(*divmod(tile, 4))
+                token(*divmod(tile, 4), parts)
+        def g_part(i):
+            if i in G_WINDOWS:
+                tile, parts = G_WINDOWS[i]
                 residual_g(*divmod(tile, 4), parts)
         def v_part(i):
             if i in V_RESIDUALS:
@@ -296,11 +308,13 @@ def tile_interfusion_pb_kernel(tc, logits1, logits2, x1, x2, out):
                 if divmod(tile, 4) not in totals:
                     open_residual(*divmod(tile, 4))
                 residual_part(*divmod(tile, 4), parts)
+        spread(*PE_CHUNKS[0])
         regroup_tile(0)
         quantise_p(0, 0)
         quantise_p(0, 1)
         regroup_tile(1)
-        quantise_tile(0)
+        quantise_x(0, 0, 0)
+        quantise_x(0, 1, 0)
         multiply(0, 0)
         for i in range(8):
             b, j = divmod(i, 4)
@@ -309,20 +323,30 @@ def tile_interfusion_pb_kernel(tc, logits1, logits2, x1, x2, out):
                 exponentials(1, 1)
             if i == 1:
                 normalise(1, 0)
+            pass
             if i == 2:
                 normalise(1, 1)
                 turn(1, 0)
                 turn(1, 1)
             regroup_tile(i + 2)
             v_part(i)
-            if i == 3:
+            if i == 3 and not True:
                 quantise_p(1, 0)
                 quantise_p(1, 1)
-            quantise_tile(i + 1)
             if i + 1 < 8:
-                multiply(*divmod(i + 1, 4))
+                nb, nj = divmod(i + 1, 4)
+                quantise_x(nb, 0, nj)
+
             if i == 0:
                 reciprocals(1, 0)
                 reciprocals(1, 1)
+            if i == 3:
+                quantise_p(1, 0)
+                quantise_p(1, 1)
+            g_token(i)
+            if i + 1 < 8:
+                quantise_x(nb, 1, nj)
+            if i + 1 < 8:
+                multiply(nb, nj)
             g_part(i)
             finish(b, j)

@@ -66,15 +66,18 @@ def tile_interfusion_pb_kernel(tc, logits1, logits2, x1, x2, out):
         sums = {}
         banks = {}
         folded = {}
+        turned = {}
 
         def load_scores(b):
             for s in range(STREAMS):
-                scores[b, s] = keep.tile([P, ROW_TILES, C], BF16, name="scores_%d_%d" % (b, s))
+                if s == 0:
+                    scores[b] = keep.tile([P, STREAMS * ROW_TILES, C], BF16, name="scores_%d" % b)
                 view = logits[s][b].rearrange("(a p) k -> p a k", p=P)
                 pieces = 2 if b == 0 else 1
                 for h in range(pieces):
                     rows = slice(h * ROW_TILES // pieces, (h + 1) * ROW_TILES // pieces)
-                    nc.sync.dma_start(out=scores[b, s][:, rows], in_=view[:, rows])
+                    first = s * ROW_TILES + h * ROW_TILES // pieces
+                    nc.sync.dma_start(out=scores[b][:, first : first + ROW_TILES // pieces], in_=view[:, rows])
 
         def load_plane(b, t):
             for s in range(STREAMS):
@@ -85,51 +88,55 @@ def tile_interfusion_pb_kernel(tc, logits1, logits2, x1, x2, out):
                     in_=maps[s][b].rearrange("(p t) h w -> p t (h w)", t=PACK)[:, t, :],
                 )
 
-        def fold(b, s, a, n, width):
+        def fold(b, a, n, width):
             first = width == C // 2
             if first:
-                folded[s, a] = soft.tile([P, n, C // 2], BF16, name="folded_%d_%d_%d" % (b, s, a))
-            source = scores[b, s][:, a : a + n] if first else folded[s, a][:]
+                folded[b, a] = soft.tile([P, n, C // 2], BF16, name="folded_%d_%d" % (b, a))
+            source = scores[b][:, a : a + n] if first else folded[b, a][:]
             nc.vector.tensor_tensor(
-                out=folded[s, a][:, :, :width],
+                out=folded[b, a][:, :, :width],
                 in0=source[:, :, :width],
                 in1=source[:, :, width : 2 * width],
                 op=ALU.max,
             )
 
-        def reduce_folded(b, s, a, n):
-            if (b, s) not in neg_max:
-                neg_max[b, s] = keep.tile([P, ROW_TILES], F32, name="neg_max_%d_%d" % (b, s))
+        def reduce_folded(b, a, n):
+            if b not in neg_max:
+                neg_max[b] = keep.tile([P, STREAMS * ROW_TILES], F32, name="neg_max_%d" % b)
             nc.vector.tensor_reduce(
-                out=neg_max[b, s][:, a : a + n], in_=folded[s, a][:, :, :FOLDED], axis=AXIS.X, op=ALU.max, negate=True
+                out=neg_max[b][:, a : a + n], in_=folded[b, a][:, :, :FOLDED], axis=AXIS.X, op=ALU.max, negate=True
             )
 
         def row_maxima(b, pieces, lag=0):
             widths = (C // 2, C // 4, C // 8)
             for step in range(len(widths) + 1 + lag * (len(pieces) - 1)):
-                for k, (s, a, n) in enumerate(pieces):
+                for k, (a, n) in enumerate(pieces):
                     at = step - lag * k
                     if 0 <= at < len(widths):
-                        fold(b, s, a, n, widths[at])
+                        fold(b, a, n, widths[at])
                     elif at == len(widths):
-                        reduce_folded(b, s, a, n)
+                        reduce_folded(b, a, n)
 
         def exponentials(b, s):
             exps[b, s] = soft.tile([P, ROW_TILES, C], F32, name="exps_%d" % s)
-            row_sum[b, s] = keep.tile([P, ROW_TILES], F32, name="row_sum_%d_%d" % (b, s))
+            if s == 0:
+                row_sum[b] = keep.tile([P, STREAMS * ROW_TILES], F32, name="row_sum_%d" % b)
             for a in range(ROW_TILES):
+                row = s * ROW_TILES + a
                 nc.scalar.activation(
                     out=exps[b, s][:, a, :],
-                    in_=scores[b, s][:, a, :],
+                    in_=scores[b][:, row, :],
                     func=ACT.Exp,
-                    bias=neg_max[b, s][:, a : a + 1],
+                    bias=neg_max[b][:, row : row + 1],
                     scale=1.0,
-                    accum_out=row_sum[b, s][:, a : a + 1],
+                    accum_out=row_sum[b][:, row : row + 1],
                 )
 
-        def reciprocals(b, s):
-            inv_sum[b, s] = keep.tile([P, ROW_TILES], F32, name="inv_sum_%d_%d" % (b, s))
-            nc.vector.reciprocal(out=inv_sum[b, s][:], in_=row_sum[b, s][:])
+        def reciprocals(b, streams):
+            if b not in inv_sum:
+                inv_sum[b] = keep.tile([P, STREAMS * ROW_TILES], F32, name="inv_sum_%d" % b)
+            rows = slice(streams[0] * ROW_TILES, (streams[-1] + 1) * ROW_TILES)
+            nc.vector.reciprocal(out=inv_sum[b][:, rows], in_=row_sum[b][:, rows])
 
         def normalise(b, s):
             probs[b, s] = soft.tile([P, ROW_TILES, C], BF16, name="probs_%d" % s)
@@ -138,27 +145,35 @@ def tile_interfusion_pb_kernel(tc, logits1, logits2, x1, x2, out):
                     out=probs[b, s][:, a, :],
                     in_=exps[b, s][:, a, :],
                     func=ACT.Copy,
-                    scale=inv_sum[b, s][:, a : a + 1],
+                    scale=inv_sum[b][:, s * ROW_TILES + a : s * ROW_TILES + a + 1],
                 )
 
-        def turn(b, s):
-            p_grouped[b, s] = soft.tile([P, C, PACK], BF16, name="p_grouped_%d" % s, align_bytes=64)
+        def turn_words(b, s):
             for half in range(2):
-                turned = turn_banks.tile([P, 2, 2, P], F32, name="turned")
+                turned[b, s, half] = turn_banks.tile([P, 2, 2, P], F32, name="turned")
                 for a in range(2):
                     words = probs[b, s][:, 2 * half + a, :].bitcast(F32)
                     for u in range(2):
-                        nc.tensor.transpose(turned[:, u, a, :], words[:, u::2], identity[:])
+                        nc.tensor.transpose(turned[b, s, half][:, u, a, :], words[:, u::2], identity[:])
+
+        def collect_words(b, s):
+            if s == 0:
+                p_grouped[b] = soft.tile([P, STREAMS, C, PACK], BF16, name="p_grouped", align_bytes=64)
+            for half in range(2):
                 nc.scalar.copy(
-                    out=p_grouped[b, s][:, 2 * half * P : 2 * (half + 1) * P, :].rearrange("p c t -> p (c t)").bitcast(F32).rearrange("p (c u) -> p c u", u=2),
-                    in_=turned[:].rearrange("p u a c -> p (a c) u"),
+                    out=p_grouped[b][:, s, 2 * half * P : 2 * (half + 1) * P, :].rearrange("p c t -> p (c t)").bitcast(F32).rearrange("p (c u) -> p c u", u=2),
+                    in_=turned[b, s, half][:].rearrange("p u a c -> p (a c) u"),
                 )
 
-        def quantise_p(b, s):
-            p_codes[b, s] = work.tile([P, C], U32, name="p_codes_%d" % s, align_bytes=64)
-            p_scales[b, s] = work.tile([P, C], U8, name="p_scales_%d" % s, align_bytes=64)
+        def turn(b, s):
+            turn_words(b, s)
+            collect_words(b, s)
+
+        def quantise_p(b):
+            p_codes[b] = work.tile([P, STREAMS * C], U32, name="p_codes", align_bytes=64)
+            p_scales[b] = work.tile([P, STREAMS * C], U8, name="p_scales", align_bytes=64)
             nc.vector.quantize_mx(
-                out=p_codes[b, s][:].bitcast(FP8X4), scales=p_scales[b, s][:], in_=p_grouped[b, s][:].rearrange("p c t -> p (c t)")
+                out=p_codes[b][:].bitcast(FP8X4), scales=p_scales[b][:], in_=p_grouped[b][:].rearrange("p s c t -> p (s c t)")
             )
 
         def spread(b, s, j):
@@ -176,28 +191,31 @@ def tile_interfusion_pb_kernel(tc, logits1, logits2, x1, x2, out):
                         stop=True,
                     )
 
+        def grouped_half(b, s, j):
+            if (b, j) not in grouped:
+                grouped[b, j] = regroup.tile([P, STREAMS, PACK * TILE], BF16, name="grouped", align_bytes=64)
+            return grouped[b, j][:, s]
+
         def group_pe(b, s, j):
-            grouped[b, s, j] = regroup.tile([P, PACK * TILE], BF16, name="grouped_scalar", align_bytes=64)
-            target = grouped[b, s, j][:].rearrange("p (r m t) -> p r m t", r=QUARTERS, t=PACK)
+            target = grouped_half(b, s, j).rearrange("p (r m t) -> p r m t", r=QUARTERS, t=PACK)
             for i in range(2):
                 nc.scalar.copy(out=target[:, :, i * P // 2 : (i + 1) * P // 2], in_=banks[b, s, j, i][:])
 
         def group(b, s, j, on_vector):
-            grouped[b, s, j] = regroup.tile(
-                [P, PACK * TILE], BF16, name="grouped_vector" if on_vector else "grouped_scalar", align_bytes=64
-            )
             source = x_maps[b, s][:].rearrange("p t (m q r) -> p q m t r", q=PACK, r=QUARTERS)[:, j]
-            target = grouped[b, s, j][:].rearrange("p (r m t) -> p m t r", r=QUARTERS, t=PACK)
+            target = grouped_half(b, s, j).rearrange("p (r m t) -> p m t r", r=QUARTERS, t=PACK)
             if on_vector:
                 nc.vector.tensor_copy(out=target, in_=source)
             else:
                 nc.scalar.copy(out=target, in_=source)
 
-        def quantise_x(b, s, j):
-            x_codes[b, s, j] = codes_pool.tile([P, TILE], U32, name="x_codes_%d" % s, align_bytes=64)
-            x_scales[b, s, j] = codes_pool.tile([P, TILE], U8, name="x_scales_%d" % s, align_bytes=64)
+        def quantise_x(b, j):
+            x_codes[b, j] = codes_pool.tile([P, STREAMS * TILE], U32, name="x_codes", align_bytes=64)
+            x_scales[b, j] = codes_pool.tile([P, STREAMS * TILE], U8, name="x_scales", align_bytes=64)
             nc.vector.quantize_mx(
-                out=x_codes[b, s, j][:].bitcast(FP8X4), scales=x_scales[b, s, j][:], in_=grouped[b, s, j][:]
+                out=x_codes[b, j][:].bitcast(FP8X4),
+                scales=x_scales[b, j][:],
+                in_=grouped[b, j][:].rearrange("p s n -> p (s n)"),
             )
 
         def residual(b, j, parts=1):
@@ -232,13 +250,14 @@ def tile_interfusion_pb_kernel(tc, logits1, logits2, x1, x2, out):
                 sums[b, j, r] = sum_banks.tile([P, C], F32, name="sums")
             for r in range(QUARTERS):
                 for s in range(STREAMS):
-                    m_cols = slice(r * P, (r + 1) * P)
+                    m_cols = slice(s * TILE + r * P, s * TILE + (r + 1) * P)
+                    c_cols = slice(s * C, (s + 1) * C)
                     nc.tensor.matmul_mx(
                         out=sums[b, j, r][:],
-                        lhsT=x_codes[b, s, j][:, m_cols].bitcast(FP8X4),
-                        lhsT_scale=x_scales[b, s, j][:, m_cols],
-                        rhs=p_codes[b, s][:].bitcast(FP8X4),
-                        rhs_scale=p_scales[b, s][:],
+                        lhsT=x_codes[b, j][:, m_cols].bitcast(FP8X4),
+                        lhsT_scale=x_scales[b, j][:, m_cols],
+                        rhs=p_codes[b][:, c_cols].bitcast(FP8X4),
+                        rhs_scale=p_scales[b][:, c_cols],
                         start=(s == 0),
                         stop=(s == STREAMS - 1),
                     )
@@ -261,19 +280,19 @@ def tile_interfusion_pb_kernel(tc, logits1, logits2, x1, x2, out):
             load_plane(0, t)
         for t in range(4):
             load_plane(1, t)
-        row_maxima(0, [(0, 0, 2), (0, 2, 2)], 1)
-        row_maxima(0, [(1, 0, 2), (1, 2, 2)], 0)
+        row_maxima(0, [(0, 2), (2, 2)], 1)
+        row_maxima(0, [(4, 2), (6, 2)], 0)
         exponentials(0, 0)
         exponentials(0, 1)
         residual(0, 0)
-        reciprocals(0, 0)
+        reciprocals(0, (0,))
         normalise(0, 0)
         turn(0, 0)
         residual(0, 1)
-        reciprocals(0, 1)
+        reciprocals(0, (1,))
         normalise(0, 1)
         turn(0, 1)
-        row_maxima(1, [(0, 0, 4), (1, 0, 4)])
+        row_maxima(1, [(0, 4), (4, 4)])
         residual(0, 2)
         residual(0, 3)
 
@@ -310,11 +329,9 @@ def tile_interfusion_pb_kernel(tc, logits1, logits2, x1, x2, out):
                 residual_part(*divmod(tile, 4), parts)
         spread(*PE_CHUNKS[0])
         regroup_tile(0)
-        quantise_p(0, 0)
-        quantise_p(0, 1)
+        quantise_p(0)
         regroup_tile(1)
-        quantise_x(0, 0, 0)
-        quantise_x(0, 1, 0)
+        quantise_x(0, 0)
         multiply(0, 0)
         for i in range(8):
             b, j = divmod(i, 4)
@@ -323,29 +340,22 @@ def tile_interfusion_pb_kernel(tc, logits1, logits2, x1, x2, out):
                 exponentials(1, 1)
             if i == 1:
                 normalise(1, 0)
-            pass
-            if i == 2:
                 normalise(1, 1)
+            regroup_tile(i + 2)
+            if i == 1:
                 turn(1, 0)
                 turn(1, 1)
-            regroup_tile(i + 2)
             v_part(i)
-            if i == 3 and not True:
-                quantise_p(1, 0)
-                quantise_p(1, 1)
             if i + 1 < 8:
                 nb, nj = divmod(i + 1, 4)
-                quantise_x(nb, 0, nj)
 
             if i == 0:
-                reciprocals(1, 0)
-                reciprocals(1, 1)
+                reciprocals(1, (0, 1))
             if i == 3:
-                quantise_p(1, 0)
-                quantise_p(1, 1)
+                quantise_p(1)
             g_token(i)
             if i + 1 < 8:
-                quantise_x(nb, 1, nj)
+                quantise_x(nb, nj)
             if i + 1 < 8:
                 multiply(nb, nj)
             g_part(i)

@@ -21,7 +21,6 @@ N = 2048
 ROW_TILES = C // P
 QUARTERS = N // C
 TILE = C
-FOLDED = 64
 
 FLOPS = 2 * STREAMS * BATCH * C * C * N
 
@@ -100,22 +99,21 @@ def tile_interfusion_pb_kernel(tc, logits1, logits2, x1, x2, out):
                 op=ALU.max,
             )
 
-        def reduce_folded(b, a, n):
+        def reduce_folded(b, a, n, width):
             if b not in neg_max:
                 neg_max[b] = keep.tile([P, STREAMS * ROW_TILES], F32, name="neg_max_%d" % b)
             nc.vector.tensor_reduce(
-                out=neg_max[b][:, a : a + n], in_=folded[b, a][:, :, :FOLDED], axis=AXIS.X, op=ALU.max, negate=True
+                out=neg_max[b][:, a : a + n], in_=folded[b, a][:, :, :width], axis=AXIS.X, op=ALU.max, negate=True
             )
 
-        def row_maxima(b, pieces, lag=0):
-            widths = (C // 2, C // 4, C // 8)
+        def row_maxima(b, pieces, widths, lag=0):
             for step in range(len(widths) + 1 + lag * (len(pieces) - 1)):
                 for k, (a, n) in enumerate(pieces):
                     at = step - lag * k
                     if 0 <= at < len(widths):
                         fold(b, a, n, widths[at])
                     elif at == len(widths):
-                        reduce_folded(b, a, n)
+                        reduce_folded(b, a, n, widths[-1])
 
         def exponentials(b, s):
             exps[b, s] = soft.tile([P, ROW_TILES, C], F32, name="exps_%d" % s)
@@ -230,11 +228,10 @@ def tile_interfusion_pb_kernel(tc, logits1, logits2, x1, x2, out):
             totals[b, j] = results.tile([P, N], F32, name="total")
 
         def residual_part(b, j, parts):
-            for i in parts:
-                cols = slice(i * C, (i + 1) * C)
-                nc.vector.tensor_tensor(
-                    out=totals[b, j][:, cols], in0=x_maps[b, 0][:, j, cols], in1=x_maps[b, 1][:, j, cols], op=ALU.add
-                )
+            cols = slice(parts[0] * C, (parts[-1] + 1) * C)
+            nc.vector.tensor_tensor(
+                out=totals[b, j][:, cols], in0=x_maps[b, 0][:, j, cols], in1=x_maps[b, 1][:, j, cols], op=ALU.add
+            )
 
         def token(b, j, parts):
             nc.vector.memset(totals[b, j][:, parts[0] * C : parts[0] * C + 1], 0.0)
@@ -280,8 +277,8 @@ def tile_interfusion_pb_kernel(tc, logits1, logits2, x1, x2, out):
             load_plane(0, t)
         for t in range(4):
             load_plane(1, t)
-        row_maxima(0, [(0, 2), (2, 2)], 1)
-        row_maxima(0, [(4, 2), (6, 2)], 0)
+        row_maxima(0, [(0, 2), (2, 2)], (C // 2, C // 4), 1)
+        row_maxima(0, [(4, 2), (6, 2)], (C // 2, C // 4), 0)
         exponentials(0, 0)
         exponentials(0, 1)
         residual(0, 0)
@@ -292,12 +289,12 @@ def tile_interfusion_pb_kernel(tc, logits1, logits2, x1, x2, out):
         reciprocals(0, (1,))
         normalise(0, 1)
         turn(0, 1)
-        row_maxima(1, [(0, 4), (4, 4)])
+        row_maxima(1, [(0, 4), (4, 4)], (C // 2, C // 4))
         residual(0, 2)
         residual(0, 3)
 
         PE_CHUNKS = ((0, 0, 1), (0, 0, 2), (0, 0, 3), (1, 0, 0), (1, 0, 1), (1, 0, 2))
-        V_CHUNKS = ((0, 1, 0), (0, 1, 1), (0, 1, 2), (0, 1, 3), (1, 1, 0))
+        V_CHUNKS = ((0, 1, 0), (0, 1, 1), (0, 1, 2), (0, 1, 3))
         G_WINDOWS = {0: (4, (0, 1)), 1: (4, (2, 3)), 2: (5, (0, 1)), 3: (5, (2, 3)), 4: (6, (0, 1)), 5: (6, (2, 3)), 6: (7, (2, 3))}
         V_RESIDUALS = {3: (7, (0, 1))}
         def regroup_tile(i):
@@ -309,7 +306,7 @@ def tile_interfusion_pb_kernel(tc, logits1, logits2, x1, x2, out):
                         k = PE_CHUNKS.index((b, s, j)) + 1
                         if k < len(PE_CHUNKS):
                             spread(*PE_CHUNKS[k])
-                    else:
+                    elif (b, s, j) != (1, 1, 0):
                         group(b, s, j, (b, s, j) in V_CHUNKS)
         def g_token(i):
             if i in G_WINDOWS:
@@ -343,6 +340,7 @@ def tile_interfusion_pb_kernel(tc, logits1, logits2, x1, x2, out):
                 normalise(1, 1)
             regroup_tile(i + 2)
             if i == 1:
+                group(1, 1, 0, False)
                 turn(1, 0)
                 turn(1, 1)
             v_part(i)

@@ -293,8 +293,8 @@ def tile_interfusion_pb_kernel(tc, logits1, logits2, x1, x2, out):
         residual(0, 2)
         residual(0, 3)
 
-        PE_CHUNKS = ((0, 0, 1), (0, 0, 2), (0, 0, 3), (1, 0, 0), (1, 0, 1), (1, 0, 2))
-        V_CHUNKS = ((0, 1, 0), (0, 1, 1), (0, 1, 2), (0, 1, 3))
+        PE_CHUNKS = ((0, 0, 1), (0, 0, 2), (1, 0, 0), (1, 0, 1), (1, 0, 2))
+        V_CHUNKS = ((0, 1, 0), (0, 1, 1), (0, 1, 2), (0, 1, 3), (1, 1, 0))
         G_WINDOWS = {0: (4, (0, 1)), 1: (4, (2, 3)), 2: (5, (0, 1)), 3: (5, (2, 3)), 4: (6, (0, 1)), 5: (6, (2, 3)), 6: (7, (2, 3))}
         V_RESIDUALS = {3: (7, (0, 1))}
         def regroup_tile(i):
@@ -306,7 +306,7 @@ def tile_interfusion_pb_kernel(tc, logits1, logits2, x1, x2, out):
                         k = PE_CHUNKS.index((b, s, j)) + 1
                         if k < len(PE_CHUNKS):
                             spread(*PE_CHUNKS[k])
-                    elif (b, s, j) != (1, 1, 0):
+                    else:
                         group(b, s, j, (b, s, j) in V_CHUNKS)
         def g_token(i):
             if i in G_WINDOWS:
@@ -340,7 +340,6 @@ def tile_interfusion_pb_kernel(tc, logits1, logits2, x1, x2, out):
                 normalise(1, 1)
             regroup_tile(i + 2)
             if i == 1:
-                group(1, 1, 0, False)
                 turn(1, 0)
                 turn(1, 1)
             v_part(i)

from contextlib import ExitStack

import concourse.mybir as mybir
from concourse.masks import make_identity

F32 = mybir.dt.float32
BF16 = mybir.dt.bfloat16
U32 = mybir.dt.uint32
U8 = mybir.dt.uint8
FP8X4 = mybir.dt.float8_e4m3fn_x4
ALU = mybir.AluOpType
ACT = mybir.ActivationFunctionType
AXIS = mybir.AxisListType

P = 128
PACK = 4
BATCH = 2
STREAMS = 2
C = 512
N = 2048
ROW_TILES = C // P
QUARTERS = N // C
TILE = C

FLOPS = 2 * STREAMS * BATCH * C * C * N


def tile_interfusion_pb_kernel(tc, logits1, logits2, x1, x2, out):
    nc = tc.nc
    logits = (logits1, logits2)
    maps = (x1, x2)
    with ExitStack() as stack:
        keep = stack.enter_context(tc.tile_pool(name="keep", bufs=1))
        work = stack.enter_context(tc.tile_pool(name="work", bufs=2))
        soft = stack.enter_context(tc.tile_pool(name="soft", bufs=1))
        regroup = stack.enter_context(tc.tile_pool(name="regroup", bufs=4))
        codes_pool = stack.enter_context(tc.tile_pool(name="codes_pool", bufs=4))
        results = stack.enter_context(tc.tile_pool(name="results", bufs=6))
        turn_banks = stack.enter_context(tc.psum_pool(name="turn_banks", bufs=2))
        sum_banks = stack.enter_context(tc.psum_pool(name="sum_banks", bufs=4))
        stack.enter_context(tc.manual_schedule())

        identity = keep.tile([P, P], F32, name="identity")
        make_identity(nc, identity[:])
        identity16 = keep.tile([P, P], BF16, name="identity16")
        make_identity(nc, identity16[:])
        warm = keep.tile([P, 1], F32, name="warm")
        nc.gpsimd.memset(warm[:], 0.0)
        nc.scalar.activation(out=warm[:], in_=warm[:], func=ACT.Exp)

        scores = {}
        x_maps = {}
        neg_max = {}
        exps = {}
        row_sum = {}
        inv_sum = {}
        probs = {}
        p_grouped = {}
        p_codes = {}
        p_scales = {}
        grouped = {}
        x_codes = {}
        x_scales = {}
        totals = {}
        sums = {}
        banks = {}
        folded = {}
        turned = {}

        def load_scores(b):
            for s in range(STREAMS):
                if s == 0:
                    scores[b] = keep.tile([P, STREAMS * ROW_TILES, C], BF16, name="scores_%d" % b)
                view = logits[s][b].rearrange("(a p) k -> p a k", p=P)
                pieces = 2 if b == 0 else 1
                for h in range(pieces):
                    rows = slice(h * ROW_TILES // pieces, (h + 1) * ROW_TILES // pieces)
                    first = s * ROW_TILES + h * ROW_TILES // pieces
                    nc.sync.dma_start(out=scores[b][:, first : first + ROW_TILES // pieces], in_=view[:, rows])

        def load_plane(b, t):
            for s in range(STREAMS):
                if t == 0:
                    x_maps[b, s] = keep.tile([P, PACK, N], BF16, name="x_map_%d_%d" % (b, s))
                nc.sync.dma_start(
                    out=x_maps[b, s][:, t, :],
                    in_=maps[s][b].rearrange("(p t) h w -> p t (h w)", t=PACK)[:, t, :],
                )

        def fold(b, a, n, width):
            first = width == C // 2
            if first:
                folded[b, a] = soft.tile([P, n, C // 2], BF16, name="folded_%d_%d" % (b, a))
            source = scores[b][:, a : a + n] if first else folded[b, a][:]
            nc.vector.tensor_tensor(
                out=folded[b, a][:, :, :width],
                in0=source[:, :, :width],
                in1=source[:, :, width : 2 * width],
                op=ALU.max,
            )

        def reduce_folded(b, a, n, width):
            if b not in neg_max:
                neg_max[b] = keep.tile([P, STREAMS * ROW_TILES], F32, name="neg_max_%d" % b)
            nc.vector.tensor_reduce(
                out=neg_max[b][:, a : a + n], in_=folded[b, a][:, :, :width], axis=AXIS.X, op=ALU.max, negate=True
            )

        def row_maxima(b, pieces, widths, lag=0):
            for step in range(len(widths) + 1 + lag * (len(pieces) - 1)):
                for k, (a, n) in enumerate(pieces):
                    at = step - lag * k
                    if 0 <= at < len(widths):
                        fold(b, a, n, widths[at])
                    elif at == len(widths):
                        reduce_folded(b, a, n, widths[-1])

        def exponentials(b, s):
            exps[b, s] = soft.tile([P, ROW_TILES, C], F32, name="exps_%d" % s)
            if s == 0:
                row_sum[b] = keep.tile([P, STREAMS * ROW_TILES], F32, name="row_sum_%d" % b)
            for a in range(ROW_TILES):
                row = s * ROW_TILES + a
                nc.scalar.activation(
                    out=exps[b, s][:, a, :],
                    in_=scores[b][:, row, :],
                    func=ACT.Exp,
                    bias=neg_max[b][:, row : row + 1],
                    scale=1.0,
                    accum_out=row_sum[b][:, row : row + 1],
                )

        def reciprocals(b, streams):
            if b not in inv_sum:
                inv_sum[b] = keep.tile([P, STREAMS * ROW_TILES], F32, name="inv_sum_%d" % b)
            rows = slice(streams[0] * ROW_TILES, (streams[-1] + 1) * ROW_TILES)
            nc.vector.reciprocal(out=inv_sum[b][:, rows], in_=row_sum[b][:, rows])

        def normalise(b, s):
            probs[b, s] = soft.tile([P, ROW_TILES, C], BF16, name="probs_%d" % s)
            for a in range(ROW_TILES):
                nc.scalar.activation(
                    out=probs[b, s][:, a, :],
                    in_=exps[b, s][:, a, :],
                    func=ACT.Copy,
                    scale=inv_sum[b][:, s * ROW_TILES + a : s * ROW_TILES + a + 1],
                )

        def turn_words(b, s):
            for half in range(2):
                turned[b, s, half] = turn_banks.tile([P, 2, 2, P], F32, name="turned")
                for a in range(2):
                    words = probs[b, s][:, 2 * half + a, :].bitcast(F32)
                    for u in range(2):
                        nc.tensor.transpose(turned[b, s, half][:, u, a, :], words[:, u::2], identity[:])

        def collect_words(b, s):
            if s == 0:
                p_grouped[b] = soft.tile([P, STREAMS, C, PACK], BF16, name="p_grouped", align_bytes=64)
            for half in range(2):
                nc.scalar.copy(
                    out=p_grouped[b][:, s, 2 * half * P : 2 * (half + 1) * P, :].rearrange("p c t -> p (c t)").bitcast(F32).rearrange("p (c u) -> p c u", u=2),
                    in_=turned[b, s, half][:].rearrange("p u a c -> p (a c) u"),
                )

        def turn(b, s):
            turn_words(b, s)
            collect_words(b, s)

        def quantise_p(b):
            p_codes[b] = work.tile([P, STREAMS * C], U32, name="p_codes", align_bytes=64)
            p_scales[b] = work.tile([P, STREAMS * C], U8, name="p_scales", align_bytes=64)
            nc.vector.quantize_mx(
                out=p_codes[b][:].bitcast(FP8X4), scales=p_scales[b][:], in_=p_grouped[b][:].rearrange("p s c t -> p (s c t)")
            )

        def spread(b, s, j):
            source = x_maps[b, s][:].rearrange("p t (m q r) -> p q m t r", q=PACK, r=QUARTERS)[:, j]
            for i in range(2):
                banks[b, s, j, i] = turn_banks.tile([P, QUARTERS, P // 2, PACK], BF16, name="spread")
                view = banks[b, s, j, i][:].rearrange("p r m t -> p m t r")
                for h in range(2):
                    m0 = i * P // 2 + h * P // 4
                    nc.tensor.matmul(
                        out=view[:, h * P // 4 : (h + 1) * P // 4],
                        lhsT=identity16[:],
                        rhs=source[:, m0 : m0 + P // 4],
                        start=True,
                        stop=True,
                    )

        def grouped_half(b, s, j):
            if (b, j) not in grouped:
                grouped[b, j] = regroup.tile([P, STREAMS, PACK * TILE], BF16, name="grouped", align_bytes=64)
            return grouped[b, j][:, s]

        def group_pe(b, s, j):
            target = grouped_half(b, s, j).rearrange("p (r m t) -> p r m t", r=QUARTERS, t=PACK)
            for i in range(2):
                nc.scalar.copy(out=target[:, :, i * P // 2 : (i + 1) * P // 2], in_=banks[b, s, j, i][:])

        def group(b, s, j, on_vector):
            source = x_maps[b, s][:].rearrange("p t (m q r) -> p q m t r", q=PACK, r=QUARTERS)[:, j]
            target = grouped_half(b, s, j).rearrange("p (r m t) -> p m t r", r=QUARTERS, t=PACK)
            if on_vector:
                nc.vector.tensor_copy(out=target, in_=source)
            else:
                nc.scalar.copy(out=target, in_=source)

        def quantise_x(b, j):
            x_codes[b, j] = codes_pool.tile([P, STREAMS * TILE], U32, name="x_codes", align_bytes=64)
            x_scales[b, j] = codes_pool.tile([P, STREAMS * TILE], U8, name="x_scales", align_bytes=64)
            nc.vector.quantize_mx(
                out=x_codes[b, j][:].bitcast(FP8X4),
                scales=x_scales[b, j][:],
                in_=grouped[b, j][:].rearrange("p s n -> p (s n)"),
            )

        def residual(b, j, parts=1):
            totals[b, j] = results.tile([P, N], F32, name="total")
            for i in range(parts):
                cols = slice(i * N // parts, (i + 1) * N // parts)
                nc.vector.tensor_tensor(
                    out=totals[b, j][:, cols], in0=x_maps[b, 0][:, j, cols], in1=x_maps[b, 1][:, j, cols], op=ALU.add
                )

        def open_residual(b, j):
            totals[b, j] = results.tile([P, N], F32, name="total")

        def residual_part(b, j, parts):
            cols = slice(parts[0] * C, (parts[-1] + 1) * C)
            nc.vector.tensor_tensor(
                out=totals[b, j][:, cols], in0=x_maps[b, 0][:, j, cols], in1=x_maps[b, 1][:, j, cols], op=ALU.add
            )

        def token(b, j, parts):
            nc.vector.memset(totals[b, j][:, parts[0] * C : parts[0] * C + 1], 0.0)

        def residual_g(b, j, parts):
            cols = slice(parts[0] * C, (parts[-1] + 1) * C)
            nc.gpsimd.tensor_tensor(
                out=totals[b, j][:, cols], in0=x_maps[b, 0][:, j, cols], in1=x_maps[b, 1][:, j, cols], op=ALU.add
            )

        def multiply(b, j):
            for r in range(QUARTERS):
                sums[b, j, r] = sum_banks.tile([P, C], F32, name="sums")
            for r in range(QUARTERS):
                for s in range(STREAMS):
                    m_cols = slice(s * TILE + r * P, s * TILE + (r + 1) * P)
                    c_cols = slice(s * C, (s + 1) * C)
                    nc.tensor.matmul_mx(
                        out=sums[b, j, r][:],
                        lhsT=x_codes[b, j][:, m_cols].bitcast(FP8X4),
                        lhsT_scale=x_scales[b, j][:, m_cols],
                        rhs=p_codes[b][:, c_cols].bitcast(FP8X4),
                        rhs_scale=p_scales[b][:, c_cols],
                        start=(s == 0),
                        stop=(s == STREAMS - 1),
                    )

        def finish(b, j):
            for r in range(QUARTERS):
                cols = slice(r * C, (r + 1) * C)
                nc.vector.tensor_tensor(
                    out=totals[b, j][:, cols], in0=sums[b, j, r][:], in1=totals[b, j][:, cols], op=ALU.add
                )
                nc.sync.dma_start(
                    out=out[b].rearrange("(p t) h w -> p t (h w)", t=PACK)[:, j, cols], in_=totals[b, j][:, cols]
                )

        load_scores(0)
        load_plane(0, 0)
        load_plane(0, 1)
        load_scores(1)
        for t in range(2, 4):
            load_plane(0, t)
        for t in range(4):
            load_plane(1, t)
        row_maxima(0, [(0, 2), (2, 2)], (C // 2, C // 4), 1)
        row_maxima(0, [(4, 2), (6, 2)], (C // 2, C // 4), 0)
        exponentials(0, 0)
        exponentials(0, 1)
        residual(0, 0)
        reciprocals(0, (0,))
        normalise(0, 0)
        turn(0, 0)
        residual(0, 1)
        reciprocals(0, (1,))
        normalise(0, 1)
        turn(0, 1)
        row_maxima(1, [(0, 4), (4, 4)], (C // 2, C // 4))
        residual(0, 2)
        residual(0, 3)

        PE_CHUNKS = ((0, 0, 1), (0, 0, 2), (1, 0, 0), (1, 0, 1), (1, 0, 2))
        V_CHUNKS = ((0, 1, 0), (0, 1, 1), (0, 1, 2), (0, 1, 3), (1, 1, 0))
        G_WINDOWS = {0: (4, (0, 1)), 1: (4, (2, 3)), 2: (5, (0, 1)), 3: (5, (2, 3)), 4: (6, (0, 1)), 5: (6, (2, 3)), 6: (7, (2, 3))}
        V_RESIDUALS = {3: (7, (0, 1))}
        def regroup_tile(i):
            if i < 8:
                b, j = divmod(i, 4)
                for s in (1, 0):
                    if (b, s, j) in PE_CHUNKS:
                        group_pe(b, s, j)
                        k = PE_CHUNKS.index((b, s, j)) + 1
                        if k < len(PE_CHUNKS):
                            spread(*PE_CHUNKS[k])
                    else:
                        group(b, s, j, (b, s, j) in V_CHUNKS)
        def g_token(i):
            if i in G_WINDOWS:
                tile, parts = G_WINDOWS[i]
                if divmod(tile, 4) not in totals:
                    open_residual(*divmod(tile, 4))
                token(*divmod(tile, 4), parts)
        def g_part(i):
            if i in G_WINDOWS:
                tile, parts = G_WINDOWS[i]
                residual_g(*divmod(tile, 4), parts)
        def v_part(i):
            if i in V_RESIDUALS:
                tile, parts = V_RESIDUALS[i]
                if divmod(tile, 4) not in totals:
                    open_residual(*divmod(tile, 4))
                residual_part(*divmod(tile, 4), parts)
        spread(*PE_CHUNKS[0])
        regroup_tile(0)
        quantise_p(0)
        regroup_tile(1)
        quantise_x(0, 0)
        multiply(0, 0)
        for i in range(8):
            b, j = divmod(i, 4)
            if i == 0:
                exponentials(1, 0)
                exponentials(1, 1)
            if i == 1:
                normalise(1, 0)
                normalise(1, 1)
            regroup_tile(i + 2)
            if i == 1:
                turn(1, 0)
                turn(1, 1)
            v_part(i)
            if i + 1 < 8:
                nb, nj = divmod(i + 1, 4)

            if i == 0:
                reciprocals(1, (0, 1))
            if i == 3:
                quantise_p(1)
            g_token(i)
            if i + 1 < 8:
                quantise_x(nb, nj)
            if i + 1 < 8:
                multiply(nb, nj)
            g_part(i)
            finish(b, j)
